import numpy as np
import ml_dtypes


def mxq(x, axis, fmt="e4m3"):
    dtype, down = {"e4m3": (ml_dtypes.float8_e4m3fn, 7), "e5m2": (ml_dtypes.float8_e5m2, 14)}[fmt]
    v = np.moveaxis(np.asarray(x, np.float32).astype(ml_dtypes.bfloat16).astype(np.float64), axis, -1)
    blocks = v.reshape(v.shape[:-1] + (-1, 32))
    amax = np.abs(blocks).max(-1, keepdims=True)
    byte = np.maximum(np.where(amax > 0, np.frexp(amax)[1] - 1 + 127, 0) - down, 1)
    scale = np.exp2(byte - 127.0)
    codes = (blocks / scale).astype(np.float32).astype(dtype).astype(np.float64)
    return np.moveaxis((codes * scale).reshape(v.shape), -1, axis)


WIDE = False


def mx_kscale(k):
    if not WIDE:
        return np.ones(k)
    levels = np.array([10, -10, 5, -5, 0])
    if k % 512:
        return np.exp2(np.random.permutation(np.resize(levels, k // 32))).repeat(32)
    a = np.empty((k // 512, 16))
    for p in range(k // 512):
        a[p, :8] = np.random.permutation(np.resize(levels, 8))
        for g in range(8):
            far = levels[np.abs(levels - a[p, g]) >= 10]
            a[p, g + 8] = far[np.random.randint(len(far))]
    return np.exp2(a.ravel()).repeat(32)


BF16 = ml_dtypes.bfloat16


def bf(x):
    return np.asarray(x, np.float32).astype(BF16)


def f64(x):
    return np.asarray(x).astype(np.float64)


B, S, D, DFF, R = 4, 128, 1024, 4096, 512


def erf(z):
    z2 = z * z
    acc = np.zeros_like(z)
    for c in (np.arange(13) + 0.5) ** 2 * 0.25:
        acc += np.exp(-c) / (c + z2)
    return np.tanh(2.0 * np.pi * z) - z * np.exp(-z2) / np.pi * acc


def gelu_erf(v):
    return 0.5 * v * (1.0 + erf(v / np.sqrt(2.0)))


def setup_inputs():
    s, r = mx_kscale(D), mx_kscale(R)
    return {"x": bf(np.random.standard_normal((B, S, D)) * s),
            "c_fc_U": bf(np.random.standard_normal((D, R)) * 2.0 / np.sqrt(D) / s[:, None]),
            "c_fc_S": bf(np.random.uniform(size=R) * r),
            "c_fc_V": bf(np.random.standard_normal((DFF, R)) / np.sqrt(R) / r[None, :]),
            "c_fc_bias": bf(np.random.standard_normal(DFF) * 0.3)}


def reference(x, c_fc_U, c_fc_S, c_fc_V, c_fc_bias):
    us = f64(c_fc_U) * f64(c_fc_S)[None, :]
    w = f64(bf(mxq(us, 1, "e4m3") @ mxq(f64(c_fc_V), 1, "e4m3").T))
    h = (mxq(f64(x), 2, "e4m3") @ mxq(w, 0, "e4m3")) + f64(c_fc_bias)
    return gelu_erf(h)

@@ -1,0 +1,218 @@
+from contextlib import ExitStack
+
+import concourse.mybir as mybir
+from concourse.masks import make_identity
+
+F32 = mybir.dt.float32
+BF16 = mybir.dt.bfloat16
+U32 = mybir.dt.uint32
+U8 = mybir.dt.uint8
+FP8X4 = mybir.dt.float8_e4m3fn_x4
+ACT = mybir.ActivationFunctionType
+ALU = mybir.AluOpType
+
+TOKENS, D, DFF, R = 512, 1024, 4096, 512
+P = 128
+CHUNK = 512
+N_CHUNKS = DFF // CHUNK
+FLOPS = 2 * D * DFF * R + 2 * TOKENS * DFF * D
+
+W_BANK_DTYPE = BF16
+VECTOR_W_TILES = (0, 2, 5)
+N_SLOTS = 4 * N_CHUNKS
+LAG = 6
+X_SLOT = 2
+
+
+def tile_hybridsuperlayer_pa_kernel(tc, x, c_fc_U, c_fc_S, c_fc_V, c_fc_bias, out):
+    nc = tc.nc
+    x_rows = x.flatten_outer_dims()
+    out_rows = out.flatten_outer_dims()
+    u_view = c_fc_U.rearrange("(g m t) r -> g m t r", g=2, t=4)
+    v_view = c_fc_V.rearrange("(c p j) r -> c p j r", c=N_CHUNKS, j=4)
+
+    with ExitStack() as ctx:
+        keep = ctx.enter_context(tc.tile_pool(name="keep", bufs=1))
+        vg_pool = ctx.enter_context(tc.tile_pool(name="vg", bufs=2))
+        vq_pool = ctx.enter_context(tc.tile_pool(name="vq", bufs=3))
+        wq_pool = ctx.enter_context(tc.tile_pool(name="wq", bufs=6))
+        ep_pool = ctx.enter_context(tc.tile_pool(name="ep", bufs=6))
+        psum = ctx.enter_context(tc.psum_pool(name="psum", bufs=8))
+        ctx.enter_context(tc.manual_schedule())
+
+        ident = keep.tile([P, P], F32)
+        make_identity(nc, ident[:])
+        warm_in = keep.tile([P, 1], F32)
+        warm_out = keep.tile([P, 1], F32)
+        nc.vector.memset(warm_in[:], 0.0)
+        nc.scalar.activation(out=warm_out[:], in_=warm_in[:], func=ACT.Gelu)
+
+        s_bc = keep.tile([P, R], BF16)
+        u_raw = [keep.tile([P, 4, R], BF16, name="u_raw%d" % g) for g in range(2)]
+        v_raw = [keep.tile([P, 4, R], BF16, name="v_raw%d" % c) for c in range(N_CHUNKS)]
+        x_raw = [keep.tile([P, D], BF16, name="x_raw%d" % i) for i in range(4)]
+        bias_bc = [keep.tile([P, DFF // 2], BF16, name="bias_bc%d" % b) for b in range(2)]
+
+        def load_v(c):
+            nc.sync.dma_start(out=v_raw[c][:], in_=v_view[c])
+
+        def load_bias(b):
+            half = DFF // 2
+            nc.sync.dma_start(out=bias_bc[b][:], in_=c_fc_bias[b * half : (b + 1) * half].partition_broadcast(P))
+
+        nc.sync.dma_start(out=s_bc[:], in_=c_fc_S.partition_broadcast(P))
+        for h in range(2):
+            nc.sync.dma_start(out=u_raw[0][:, 2 * h : 2 * h + 2, :], in_=u_view[0][:, 2 * h : 2 * h + 2, :])
+        for h in range(2):
+            nc.sync.dma_start(out=v_raw[0][:, 2 * h : 2 * h + 2, :], in_=v_view[0][:, 2 * h : 2 * h + 2, :])
+        nc.sync.dma_start(out=u_raw[1][:], in_=u_view[1])
+        load_v(1)
+        for i in range(4):
+            nc.sync.dma_start(out=x_raw[i][:], in_=x_rows[i * P : (i + 1) * P, :])
+        load_v(2)
+        load_bias(0)
+        load_v(3)
+        load_v(4)
+        load_bias(1)
+        load_v(5)
+        load_v(6)
+        load_v(7)
+
+        def copy_out(on_vector, dst, src):
+            if on_vector:
+                nc.vector.tensor_copy(out=dst, in_=src)
+            else:
+                nc.scalar.copy(out=dst, in_=src)
+
+        def transpose_bank(words):
+            bank = psum.tile([P, 2, 2, P], F32, tag="bank", name="tp_bank")
+            for s in range(2):
+                for u in range(2):
+                    nc.tensor.transpose(bank[:, s, u, :], words[s][u], ident[:])
+            return bank
+
+        def every_2nd_word(row_tile, first_word):
+            words = row_tile.bitcast(F32)
+            return [words[:, first_word + u : first_word + 256 : 2] for u in range(2)]
+
+        def quantize(grouped, name, pool):
+            codes = pool.tile([P, CHUNK], U32, tag=name + "_codes", name=name + "_codes", align_bytes=64)
+            scales = pool.tile([P, CHUNK], U8, tag=name + "_scales", name=name + "_scales", align_bytes=64)
+            nc.vector.quantize_mx(out=codes[:].bitcast(FP8X4), scales=scales[:], in_=grouped[:])
+            return codes, scales
+
+        us = [keep.tile([P, 4, R], BF16, name="us%d" % g) for g in range(2)]
+        us_grouped = [keep.tile([P, 4 * CHUNK], BF16, name="us_grouped%d" % g, align_bytes=64) for g in range(2)]
+        x_grouped = [keep.tile([P, 4 * CHUNK], BF16, name="x_grouped%d" % g, align_bytes=64) for g in range(2)]
+        us_q = {}
+        x_q = {}
+        v_grouped = {}
+        v_q = {}
+        w_grouped = {}
+        w_q = {}
+        h_tiles = {}
+
+        def scale_u(g):
+            for t in range(4):
+                nc.vector.tensor_tensor(out=us[g][:, t, :], in0=u_raw[g][:, t, :], in1=s_bc[:], op=ALU.mult)
+
+        def grouped_half(grouped, h):
+            return grouped[:, 1024 * h : 1024 * (h + 1)].bitcast(F32).rearrange("p (s m u) -> p s m u", s=2, u=2)
+
+        def transpose_u(g):
+            for h in range(2):
+                bank = transpose_bank([every_2nd_word(us[g][:, 2 * h + s, :], 0) for s in range(2)])
+                copy_out(h == 0, grouped_half(us_grouped[g], h), bank[:].rearrange("p s u m -> p s m u"))
+
+        def transpose_x(g):
+            for h in range(2):
+                bank = transpose_bank([every_2nd_word(x_raw[2 * h + s][:], 256 * g) for s in range(2)])
+                copy_out(h == 0, grouped_half(x_grouped[g], h), bank[:].rearrange("p s u m -> p s m u"))
+
+        def transpose_v(c):
+            v_grouped[c] = vg_pool.tile([P, 4 * CHUNK], BF16, tag="v_grouped", name="v_grouped", align_bytes=64)
+            dst = v_grouped[c][:].bitcast(F32).rearrange("k (p j u) -> k p j u", j=4, u=2)
+            for h in range(2):
+                bank = transpose_bank([every_2nd_word(v_raw[c][:, 2 * h + s, :], 0) for s in range(2)])
+                copy_out(False, dst[:, :, 2 * h : 2 * h + 2, :], bank[:].rearrange("k j u p -> k p j u"))
+
+        def stage1_tile(c, n):
+            g, fs = n // 4, n % 4
+            if fs == 0:
+                w_grouped[(c, g)] = wq_pool.tile([P, 4 * CHUNK], BF16, tag="w_grouped", name="w_grouped", align_bytes=64)
+            u_codes, u_scales = us_q[g]
+            v_codes, v_scales = v_q[c]
+            w_bank = psum.tile([P, 4, P], W_BANK_DTYPE, tag="bank", name="w_bank")
+            cols = slice(fs * P, (fs + 1) * P)
+            for t in range(4):
+                d_cols = slice(t * P, (t + 1) * P)
+                nc.tensor.matmul_mx(
+                    out=w_bank[:, t, :],
+                    lhsT=u_codes[:, d_cols].bitcast(FP8X4),
+                    lhsT_scale=u_scales[:, d_cols],
+                    rhs=v_codes[:, cols].bitcast(FP8X4),
+                    rhs_scale=v_scales[:, cols],
+                    start=True,
+                    stop=True,
+                )
+            dst = w_grouped[(c, g)][:, 4 * P * fs : 4 * P * (fs + 1)].rearrange("p (f t) -> p f t", t=4)
+            copy_out(n in VECTOR_W_TILES, dst, w_bank[:].rearrange("p t f -> p f t"))
+
+        def stage2_tile(k):
+            c, i = k // 4, k % 4
+            acc = psum.tile([P, CHUNK], F32, tag="bank", name="acc")
+            toks = slice(i * P, (i + 1) * P)
+            for g in range(2):
+                nc.tensor.matmul_mx(
+                    out=acc[:],
+                    lhsT=x_q[g][0][:, toks].bitcast(FP8X4),
+                    lhsT_scale=x_q[g][1][:, toks],
+                    rhs=w_q[(c, g)][0][:].bitcast(FP8X4),
+                    rhs_scale=w_q[(c, g)][1][:],
+                    start=(g == 0),
+                    stop=(g == 1),
+                )
+            h_tiles[k] = ep_pool.tile([P, CHUNK], F32, tag="h_sb", name="h_sb")
+            b = c // (N_CHUNKS // 2)
+            b_cols = slice((c % (N_CHUNKS // 2)) * CHUNK, (c % (N_CHUNKS // 2) + 1) * CHUNK)
+            nc.vector.tensor_tensor(out=h_tiles[k][:], in0=acc[:], in1=bias_bc[b][:, b_cols], op=ALU.add)
+
+        def gelu_and_store(k):
+            c, i = k // 4, k % 4
+            o_sb = ep_pool.tile([P, CHUNK], F32, tag="o_sb")
+            nc.scalar.activation(out=o_sb[:], in_=h_tiles[k][:], func=ACT.Gelu)
+            nc.sync.dma_start(out=out_rows[i * P : (i + 1) * P, c * CHUNK : (c + 1) * CHUNK], in_=o_sb[:])
+
+        scale_u(0)
+        transpose_u(0)
+        us_q[0] = quantize(us_grouped[0], "us0", keep)
+        transpose_v(0)
+        scale_u(1)
+        v_q[0] = quantize(v_grouped[0], "v", vq_pool)
+        transpose_u(1)
+        us_q[1] = quantize(us_grouped[1], "us1", keep)
+
+        for s in range(N_SLOTS + LAG):
+            if s < N_SLOTS:
+                c, q = s // 4, s % 4
+                if q == 0 and c + 1 < N_CHUNKS:
+                    transpose_v(c + 1)
+                stage1_tile(c, 2 * q)
+                stage1_tile(c, 2 * q + 1)
+                if q == 1 and c + 1 < N_CHUNKS:
+                    v_q[c + 1] = quantize(v_grouped[c + 1], "v", vq_pool)
+                if q == 2:
+                    w_q[(c, 0)] = quantize(w_grouped[(c, 0)], "w", wq_pool)
+            if 0 < s <= N_SLOTS and s % 4 == 0:
+                w_q[(s // 4 - 1, 1)] = quantize(w_grouped[(s // 4 - 1, 1)], "w", wq_pool)
+            if s == X_SLOT:
+                for g in range(2):
+                    transpose_x(g)
+                for g in range(2):
+                    x_q[g] = quantize(x_grouped[g], "x%d" % g, keep)
+            k = s - LAG
+            if k >= 0:
+                stage2_tile(k)
+                if k >= 1:
+                    gelu_and_store(k - 1)
+        gelu_and_store(N_SLOTS - 1)

@@ -14,14 +14,33 @@ ALU = mybir.AluOpType
 TOKENS, D, DFF, R = 512, 1024, 4096, 512
 P = 128
 CHUNK = 512
+HALF = 256
 N_CHUNKS = DFF // CHUNK
 FLOPS = 2 * D * DFF * R + 2 * TOKENS * DFF * D
-
-W_BANK_DTYPE = BF16
-VECTOR_W_TILES = (0, 2, 5)
 N_SLOTS = 4 * N_CHUNKS
-LAG = 6
-X_SLOT = 2
+
+LAG = 8
+A_TV = 5
+D_CW = 1
+D_CV = 0
+D_QV = 2
+D_QW = 2
+D_ADD = 1
+D_G = 2
+X_SLOTS = (1, 2)
+D_CX = 0
+D_QX = 2
+VEC_W = (1,)
+VEC_V = (1,)
+VEC_X = (0,)
+DVE_ORDER = ("add", "cw", "cv", "cx", "qw", "qv", "qx")
+ACT_ORDER = ("cw", "cv", "cx", "gelu")
+HEAD_U0 = (False, False)
+HEAD_V0 = (False, False)
+HEAD_U1 = (False, False)
+SC1_EARLY = True
+TV1_SLOT = 0
+T_AFTER = False
 
 
 def tile_hybridsuperlayer_pa_kernel(tc, x, c_fc_U, c_fc_S, c_fc_V, c_fc_bias, out):
@@ -29,7 +48,7 @@ def tile_hybridsuperlayer_pa_kernel(tc, x, c_fc_U, c_fc_S, c_fc_V, c_fc_bias, ou
     x_rows = x.flatten_outer_dims()
     out_rows = out.flatten_outer_dims()
     u_view = c_fc_U.rearrange("(g m t) r -> g m t r", g=2, t=4)
-    v_view = c_fc_V.rearrange("(c p j) r -> c p j r", c=N_CHUNKS, j=4)
+    v_view = c_fc_V.rearrange("(c h p j) r -> c h p j r", c=N_CHUNKS, h=2, j=2)
 
     with ExitStack() as ctx:
         keep = ctx.enter_context(tc.tile_pool(name="keep", bufs=1))
@@ -49,12 +68,13 @@ def tile_hybridsuperlayer_pa_kernel(tc, x, c_fc_U, c_fc_S, c_fc_V, c_fc_bias, ou
 
         s_bc = keep.tile([P, R], BF16)
         u_raw = [keep.tile([P, 4, R], BF16, name="u_raw%d" % g) for g in range(2)]
-        v_raw = [keep.tile([P, 4, R], BF16, name="v_raw%d" % c) for c in range(N_CHUNKS)]
+        v_raw = [keep.tile([P, 2, 2, R], BF16, name="v_raw%d" % c) for c in range(N_CHUNKS)]
         x_raw = [keep.tile([P, D], BF16, name="x_raw%d" % i) for i in range(4)]
         bias_bc = [keep.tile([P, DFF // 2], BF16, name="bias_bc%d" % b) for b in range(2)]
 
         def load_v(c):
-            nc.sync.dma_start(out=v_raw[c][:], in_=v_view[c])
+            for h in range(2):
+                nc.sync.dma_start(out=v_raw[c][:, h, :, :], in_=v_view[c][h])
 
         def load_bias(b):
             half = DFF // 2
@@ -63,8 +83,7 @@ def tile_hybridsuperlayer_pa_kernel(tc, x, c_fc_U, c_fc_S, c_fc_V, c_fc_bias, ou
         nc.sync.dma_start(out=s_bc[:], in_=c_fc_S.partition_broadcast(P))
         for h in range(2):
             nc.sync.dma_start(out=u_raw[0][:, 2 * h : 2 * h + 2, :], in_=u_view[0][:, 2 * h : 2 * h + 2, :])
-        for h in range(2):
-            nc.sync.dma_start(out=v_raw[0][:, 2 * h : 2 * h + 2, :], in_=v_view[0][:, 2 * h : 2 * h + 2, :])
+        load_v(0)
         nc.sync.dma_start(out=u_raw[1][:], in_=u_view[1])
         load_v(1)
         for i in range(4):
@@ -111,6 +130,7 @@ def tile_hybridsuperlayer_pa_kernel(tc, x, c_fc_U, c_fc_S, c_fc_V, c_fc_bias, ou
         w_grouped = {}
         w_q = {}
         h_tiles = {}
+        banks = {}
 
         def scale_u(g):
             for t in range(4):
@@ -119,31 +139,35 @@ def tile_hybridsuperlayer_pa_kernel(tc, x, c_fc_U, c_fc_S, c_fc_V, c_fc_bias, ou
         def grouped_half(grouped, h):
             return grouped[:, 1024 * h : 1024 * (h + 1)].bitcast(F32).rearrange("p (s m u) -> p s m u", s=2, u=2)
 
-        def transpose_u(g):
+        def tu(g):
             for h in range(2):
-                bank = transpose_bank([every_2nd_word(us[g][:, 2 * h + s, :], 0) for s in range(2)])
-                copy_out(h == 0, grouped_half(us_grouped[g], h), bank[:].rearrange("p s u m -> p s m u"))
+                banks[("u", g, h)] = transpose_bank([every_2nd_word(us[g][:, 2 * h + s, :], 0) for s in range(2)])
 
-        def transpose_x(g):
+        def cu(g, h, on_vector):
+            copy_out(on_vector, grouped_half(us_grouped[g], h), banks[("u", g, h)][:].rearrange("p s u m -> p s m u"))
+
+        def tx(g):
             for h in range(2):
-                bank = transpose_bank([every_2nd_word(x_raw[2 * h + s][:], 256 * g) for s in range(2)])
-                copy_out(h == 0, grouped_half(x_grouped[g], h), bank[:].rearrange("p s u m -> p s m u"))
+                banks[("x", g, h)] = transpose_bank([every_2nd_word(x_raw[2 * h + s][:], 256 * g) for s in range(2)])
 
-        def transpose_v(c):
+        def cx(g, h, on_vector):
+            copy_out(on_vector, grouped_half(x_grouped[g], h), banks[("x", g, h)][:].rearrange("p s u m -> p s m u"))
+
+        def tv(c):
             v_grouped[c] = vg_pool.tile([P, 4 * CHUNK], BF16, tag="v_grouped", name="v_grouped", align_bytes=64)
-            dst = v_grouped[c][:].bitcast(F32).rearrange("k (p j u) -> k p j u", j=4, u=2)
             for h in range(2):
-                bank = transpose_bank([every_2nd_word(v_raw[c][:, 2 * h + s, :], 0) for s in range(2)])
-                copy_out(False, dst[:, :, 2 * h : 2 * h + 2, :], bank[:].rearrange("k j u p -> k p j u"))
+                banks[("v", c, h)] = transpose_bank([every_2nd_word(v_raw[c][:, h, j, :], 0) for j in range(2)])
 
-        def stage1_tile(c, n):
-            g, fs = n // 4, n % 4
-            if fs == 0:
-                w_grouped[(c, g)] = wq_pool.tile([P, 4 * CHUNK], BF16, tag="w_grouped", name="w_grouped", align_bytes=64)
+        def cv(c, h, on_vector):
+            dst = v_grouped[c][:, 1024 * h : 1024 * (h + 1)].bitcast(F32).rearrange("k (p j u) -> k p j u", j=2, u=2)
+            copy_out(on_vector, dst, banks[("v", c, h)][:].rearrange("k j u p -> k p j u"))
+
+        def s1(n):
+            c, g, h = n // 4, (n % 4) // 2, n % 2
             u_codes, u_scales = us_q[g]
             v_codes, v_scales = v_q[c]
-            w_bank = psum.tile([P, 4, P], W_BANK_DTYPE, tag="bank", name="w_bank")
-            cols = slice(fs * P, (fs + 1) * P)
+            w_bank = psum.tile([P, 4, HALF], BF16, tag="bank", name="w_bank")
+            cols = slice(h * HALF, (h + 1) * HALF)
             for t in range(4):
                 d_cols = slice(t * P, (t + 1) * P)
                 nc.tensor.matmul_mx(
@@ -155,10 +179,16 @@ def tile_hybridsuperlayer_pa_kernel(tc, x, c_fc_U, c_fc_S, c_fc_V, c_fc_bias, ou
                     start=True,
                     stop=True,
                 )
-            dst = w_grouped[(c, g)][:, 4 * P * fs : 4 * P * (fs + 1)].rearrange("p (f t) -> p f t", t=4)
-            copy_out(n in VECTOR_W_TILES, dst, w_bank[:].rearrange("p t f -> p f t"))
+            banks[("w", n)] = w_bank
 
-        def stage2_tile(k):
+        def cw(n, on_vector):
+            c, g, h = n // 4, (n % 4) // 2, n % 2
+            if h == 0:
+                w_grouped[(c, g)] = wq_pool.tile([P, 4 * CHUNK], BF16, tag="w_grouped", name="w_grouped", align_bytes=64)
+            dst = w_grouped[(c, g)][:, 4 * HALF * h : 4 * HALF * (h + 1)].rearrange("p (f t) -> p f t", t=4)
+            copy_out(on_vector, dst, banks[("w", n)][:].rearrange("p t f -> p f t"))
+
+        def s2(k):
             c, i = k // 4, k % 4
             acc = psum.tile([P, CHUNK], F32, tag="bank", name="acc")
             toks = slice(i * P, (i + 1) * P)
@@ -172,47 +202,101 @@ def tile_hybridsuperlayer_pa_kernel(tc, x, c_fc_U, c_fc_S, c_fc_V, c_fc_bias, ou
                     start=(g == 0),
                     stop=(g == 1),
                 )
+            banks[("a", k)] = acc
+
+        def add(k):
+            c = k // 4
             h_tiles[k] = ep_pool.tile([P, CHUNK], F32, tag="h_sb", name="h_sb")
             b = c // (N_CHUNKS // 2)
             b_cols = slice((c % (N_CHUNKS // 2)) * CHUNK, (c % (N_CHUNKS // 2) + 1) * CHUNK)
-            nc.vector.tensor_tensor(out=h_tiles[k][:], in0=acc[:], in1=bias_bc[b][:, b_cols], op=ALU.add)
+            nc.vector.tensor_tensor(out=h_tiles[k][:], in0=banks[("a", k)][:], in1=bias_bc[b][:, b_cols], op=ALU.add)
 
-        def gelu_and_store(k):
+        def gelu(k):
             c, i = k // 4, k % 4
             o_sb = ep_pool.tile([P, CHUNK], F32, tag="o_sb")
             nc.scalar.activation(out=o_sb[:], in_=h_tiles[k][:], func=ACT.Gelu)
             nc.sync.dma_start(out=out_rows[i * P : (i + 1) * P, c * CHUNK : (c + 1) * CHUNK], in_=o_sb[:])
 
         scale_u(0)
-        transpose_u(0)
+        if SC1_EARLY:
+            scale_u(1)
+        tu(0)
+        cu(0, 0, HEAD_U0[0])
+        cu(0, 1, HEAD_U0[1])
+        tv(0)
+        cv(0, 0, HEAD_V0[0])
+        cv(0, 1, HEAD_V0[1])
         us_q[0] = quantize(us_grouped[0], "us0", keep)
-        transpose_v(0)
-        scale_u(1)
         v_q[0] = quantize(v_grouped[0], "v", vq_pool)
-        transpose_u(1)
+        if not SC1_EARLY:
+            scale_u(1)
+        tu(1)
+        cu(1, 0, HEAD_U1[0])
+        cu(1, 1, HEAD_U1[1])
         us_q[1] = quantize(us_grouped[1], "us1", keep)
 
-        for s in range(N_SLOTS + LAG):
+        def tv_slot(c):
+            return TV1_SLOT if c == 1 else 4 * c - A_TV
+
+        for s in range(N_SLOTS + LAG + 4):
+            def t_runs():
+                for c in range(1, N_CHUNKS):
+                    if tv_slot(c) == s:
+                        tv(c)
+                for g in range(2):
+                    if X_SLOTS[g] == s:
+                        tx(g)
+            if not T_AFTER:
+                t_runs()
             if s < N_SLOTS:
-                c, q = s // 4, s % 4
-                if q == 0 and c + 1 < N_CHUNKS:
-                    transpose_v(c + 1)
-                stage1_tile(c, 2 * q)
-                stage1_tile(c, 2 * q + 1)
-                if q == 1 and c + 1 < N_CHUNKS:
-                    v_q[c + 1] = quantize(v_grouped[c + 1], "v", vq_pool)
-                if q == 2:
-                    w_q[(c, 0)] = quantize(w_grouped[(c, 0)], "w", wq_pool)
-            if 0 < s <= N_SLOTS and s % 4 == 0:
-                w_q[(s // 4 - 1, 1)] = quantize(w_grouped[(s // 4 - 1, 1)], "w", wq_pool)
-            if s == X_SLOT:
-                for g in range(2):
-                    transpose_x(g)
-                for g in range(2):
-                    x_q[g] = quantize(x_grouped[g], "x%d" % g, keep)
-            k = s - LAG
-            if k >= 0:
-                stage2_tile(k)
-                if k >= 1:
-                    gelu_and_store(k - 1)
-        gelu_and_store(N_SLOTS - 1)
+                s1(s)
+            if 0 <= s - LAG < N_SLOTS:
+                s2(s - LAG)
+            if T_AFTER:
+                t_runs()
+            for what in DVE_ORDER:
+                if what == "add" and 0 <= s - LAG - D_ADD < N_SLOTS:
+                    add(s - LAG - D_ADD)
+                if what == "cw" and 0 <= s - D_CW < N_SLOTS and (s - D_CW) % 4 in VEC_W:
+                    cw(s - D_CW, True)
+                if what == "cv":
+                    for c in range(1, N_CHUNKS):
+                        if tv_slot(c) + D_CV == s:
+                            for h in VEC_V:
+                                cv(c, h, True)
+                if what == "cx":
+                    for g in range(2):
+                        if X_SLOTS[g] + D_CX == s:
+                            for h in VEC_X:
+                                cx(g, h, True)
+            for what in ACT_ORDER:
+                if what == "gelu" and 0 <= s - LAG - D_G < N_SLOTS:
+                    gelu(s - LAG - D_G)
+                if what == "cw" and 0 <= s - D_CW < N_SLOTS and (s - D_CW) % 4 not in VEC_W:
+                    cw(s - D_CW, False)
+                if what == "cv":
+                    for c in range(1, N_CHUNKS):
+                        if tv_slot(c) + D_CV == s:
+                            for h in range(2):
+                                if h not in VEC_V:
+                                    cv(c, h, False)
+                if what == "cx":
+                    for g in range(2):
+                        if X_SLOTS[g] + D_CX == s:
+                            for h in range(2):
+                                if h not in VEC_X:
+                                    cx(g, h, False)
+            for what in DVE_ORDER:
+                if what == "qw":
+                    for c in range(N_CHUNKS):
+                        for g in range(2):
+                            if 4 * c + 2 * g + 1 + D_QW == s:
+                                w_q[(c, g)] = quantize(w_grouped[(c, g)], "w", wq_pool)
+                if what == "qv":
+                    for c in range(1, N_CHUNKS):
+                        if tv_slot(c) + D_QV == s:
+                            v_q[c] = quantize(v_grouped[c], "v", vq_pool)
+                if what == "qx":
+                    for g in range(2):
+                        if X_SLOTS[g] + D_QX == s:
+                            x_q[g] = quantize(x_grouped[g], "x%d" % g, keep)

@@ -38,7 +38,7 @@ ACT_ORDER = ("cw", "cv", "cx", "gelu")
 HEAD_U0 = (False, False)
 HEAD_V0 = (False, False)
 HEAD_U1 = (False, False)
-SC1_EARLY = True
+QV0_HALVES = True
 TV1_SLOT = 0
 T_AFTER = False
 
@@ -66,7 +66,7 @@ def tile_hybridsuperlayer_pa_kernel(tc, x, c_fc_U, c_fc_S, c_fc_V, c_fc_bias, ou
         nc.vector.memset(warm_in[:], 0.0)
         nc.scalar.activation(out=warm_out[:], in_=warm_in[:], func=ACT.Gelu)
 
-        s_bc = keep.tile([P, R], BF16)
+        s4 = keep.tile([P, 1, 4], BF16)
         u_raw = [keep.tile([P, 4, R], BF16, name="u_raw%d" % g) for g in range(2)]
         v_raw = [keep.tile([P, 2, 2, R], BF16, name="v_raw%d" % c) for c in range(N_CHUNKS)]
         x_raw = [keep.tile([P, D], BF16, name="x_raw%d" % i) for i in range(4)]
@@ -80,7 +80,7 @@ def tile_hybridsuperlayer_pa_kernel(tc, x, c_fc_U, c_fc_S, c_fc_V, c_fc_bias, ou
             half = DFF // 2
             nc.sync.dma_start(out=bias_bc[b][:], in_=c_fc_bias[b * half : (b + 1) * half].partition_broadcast(P))
 
-        nc.sync.dma_start(out=s_bc[:], in_=c_fc_S.partition_broadcast(P))
+        nc.sync.dma_start(out=s4[:, 0, :], in_=c_fc_S.rearrange("(p t) -> p t", t=4))
         for h in range(2):
             nc.sync.dma_start(out=u_raw[0][:, 2 * h : 2 * h + 2, :], in_=u_view[0][:, 2 * h : 2 * h + 2, :])
         load_v(0)
@@ -120,7 +120,7 @@ def tile_hybridsuperlayer_pa_kernel(tc, x, c_fc_U, c_fc_S, c_fc_V, c_fc_bias, ou
             nc.vector.quantize_mx(out=codes[:].bitcast(FP8X4), scales=scales[:], in_=grouped[:])
             return codes, scales
 
-        us = [keep.tile([P, 4, R], BF16, name="us%d" % g) for g in range(2)]
+        u_grouped = [keep.tile([P, 4 * CHUNK], BF16, name="u_grouped%d" % g, align_bytes=64) for g in range(2)]
         us_grouped = [keep.tile([P, 4 * CHUNK], BF16, name="us_grouped%d" % g, align_bytes=64) for g in range(2)]
         x_grouped = [keep.tile([P, 4 * CHUNK], BF16, name="x_grouped%d" % g, align_bytes=64) for g in range(2)]
         us_q = {}
@@ -132,19 +132,24 @@ def tile_hybridsuperlayer_pa_kernel(tc, x, c_fc_U, c_fc_S, c_fc_V, c_fc_bias, ou
         h_tiles = {}
         banks = {}
 
-        def scale_u(g):
-            for t in range(4):
-                nc.vector.tensor_tensor(out=us[g][:, t, :], in0=u_raw[g][:, t, :], in1=s_bc[:], op=ALU.mult)
+        def scale_u(g, h):
+            cols = slice(1024 * h, 1024 * (h + 1))
+            nc.vector.tensor_tensor(
+                out=us_grouped[g][:, cols].rearrange("p (m t) -> p m t", t=4),
+                in0=u_grouped[g][:, cols].rearrange("p (m t) -> p m t", t=4),
+                in1=s4[:].to_broadcast([P, HALF, 4]),
+                op=ALU.mult,
+            )
 
         def grouped_half(grouped, h):
             return grouped[:, 1024 * h : 1024 * (h + 1)].bitcast(F32).rearrange("p (s m u) -> p s m u", s=2, u=2)
 
         def tu(g):
             for h in range(2):
-                banks[("u", g, h)] = transpose_bank([every_2nd_word(us[g][:, 2 * h + s, :], 0) for s in range(2)])
+                banks[("u", g, h)] = transpose_bank([every_2nd_word(u_raw[g][:, 2 * h + s, :], 0) for s in range(2)])
 
         def cu(g, h, on_vector):
-            copy_out(on_vector, grouped_half(us_grouped[g], h), banks[("u", g, h)][:].rearrange("p s u m -> p s m u"))
+            copy_out(on_vector, grouped_half(u_grouped[g], h), banks[("u", g, h)][:].rearrange("p s u m -> p s m u"))
 
         def tx(g):
             for h in range(2):
@@ -217,22 +222,36 @@ def tile_hybridsuperlayer_pa_kernel(tc, x, c_fc_U, c_fc_S, c_fc_V, c_fc_bias, ou
             nc.scalar.activation(out=o_sb[:], in_=h_tiles[k][:], func=ACT.Gelu)
             nc.sync.dma_start(out=out_rows[i * P : (i + 1) * P, c * CHUNK : (c + 1) * CHUNK], in_=o_sb[:])
 
-        scale_u(0)
-        if SC1_EARLY:
-            scale_u(1)
+        def quantize_v0(h):
+            if h == 0:
+                v_q[0] = (
+                    vq_pool.tile([P, CHUNK], U32, tag="v_codes", name="v_codes", align_bytes=64),
+                    vq_pool.tile([P, CHUNK], U8, tag="v_scales", name="v_scales", align_bytes=64),
+                )
+            cols = slice(HALF * h, HALF * (h + 1))
+            nc.vector.quantize_mx(
+                out=v_q[0][0][:, cols].bitcast(FP8X4), scales=v_q[0][1][:, cols], in_=v_grouped[0][:, 4 * HALF * h : 4 * HALF * (h + 1)]
+            )
+
         tu(0)
         cu(0, 0, HEAD_U0[0])
         cu(0, 1, HEAD_U0[1])
+        scale_u(0, 0)
+        scale_u(0, 1)
         tv(0)
         cv(0, 0, HEAD_V0[0])
         cv(0, 1, HEAD_V0[1])
         us_q[0] = quantize(us_grouped[0], "us0", keep)
-        v_q[0] = quantize(v_grouped[0], "v", vq_pool)
-        if not SC1_EARLY:
-            scale_u(1)
+        if QV0_HALVES:
+            quantize_v0(0)
+            quantize_v0(1)
+        else:
+            v_q[0] = quantize(v_grouped[0], "v", vq_pool)
         tu(1)
         cu(1, 0, HEAD_U1[0])
         cu(1, 1, HEAD_U1[1])
+        scale_u(1, 0)
+        scale_u(1, 1)
         us_q[1] = quantize(us_grouped[1], "us1", keep)
 
         def tv_slot(c):

@@ -39,6 +39,8 @@ HEAD_U0 = (False, False)
 HEAD_V0 = (False, False)
 HEAD_U1 = (False, False)
 QV0_HALVES = True
+BIAS_FIRST = 2
+BIAS_AHEAD = 6
 TV1_SLOT = 0
 T_AFTER = False
 
@@ -70,15 +72,14 @@ def tile_hybridsuperlayer_pa_kernel(tc, x, c_fc_U, c_fc_S, c_fc_V, c_fc_bias, ou
         u_raw = [keep.tile([P, 4, R], BF16, name="u_raw%d" % g) for g in range(2)]
         v_raw = [keep.tile([P, 2, 2, R], BF16, name="v_raw%d" % c) for c in range(N_CHUNKS)]
         x_raw = [keep.tile([P, D], BF16, name="x_raw%d" % i) for i in range(4)]
-        bias_bc = [keep.tile([P, DFF // 2], BF16, name="bias_bc%d" % b) for b in range(2)]
+        bias_bc = [keep.tile([P, CHUNK], BF16, name="bias_bc%d" % c) for c in range(N_CHUNKS)]
 
         def load_v(c):
             for h in range(2):
                 nc.sync.dma_start(out=v_raw[c][:, h, :, :], in_=v_view[c][h])
 
-        def load_bias(b):
-            half = DFF // 2
-            nc.sync.dma_start(out=bias_bc[b][:], in_=c_fc_bias[b * half : (b + 1) * half].partition_broadcast(P))
+        def load_bias(c):
+            nc.sync.dma_start(out=bias_bc[c][:], in_=c_fc_bias[c * CHUNK : (c + 1) * CHUNK].partition_broadcast(P))
 
         nc.sync.dma_start(out=s4[:, 0, :], in_=c_fc_S.rearrange("(p t) -> p t", t=4))
         for h in range(2):
@@ -89,13 +90,13 @@ def tile_hybridsuperlayer_pa_kernel(tc, x, c_fc_U, c_fc_S, c_fc_V, c_fc_bias, ou
         for i in range(4):
             nc.sync.dma_start(out=x_raw[i][:], in_=x_rows[i * P : (i + 1) * P, :])
         load_v(2)
-        load_bias(0)
         load_v(3)
         load_v(4)
-        load_bias(1)
         load_v(5)
         load_v(6)
         load_v(7)
+        for c in range(BIAS_FIRST):
+            load_bias(c)
 
         def copy_out(on_vector, dst, src):
             if on_vector:
@@ -212,9 +213,7 @@ def tile_hybridsuperlayer_pa_kernel(tc, x, c_fc_U, c_fc_S, c_fc_V, c_fc_bias, ou
         def add(k):
             c = k // 4
             h_tiles[k] = ep_pool.tile([P, CHUNK], F32, tag="h_sb", name="h_sb")
-            b = c // (N_CHUNKS // 2)
-            b_cols = slice((c % (N_CHUNKS // 2)) * CHUNK, (c % (N_CHUNKS // 2) + 1) * CHUNK)
-            nc.vector.tensor_tensor(out=h_tiles[k][:], in0=banks[("a", k)][:], in1=bias_bc[b][:, b_cols], op=ALU.add)
+            nc.vector.tensor_tensor(out=h_tiles[k][:], in0=banks[("a", k)][:], in1=bias_bc[c][:], op=ALU.add)
 
         def gelu(k):
             c, i = k // 4, k % 4
@@ -258,6 +257,9 @@ def tile_hybridsuperlayer_pa_kernel(tc, x, c_fc_U, c_fc_S, c_fc_V, c_fc_bias, ou
             return TV1_SLOT if c == 1 else 4 * c - A_TV
 
         for s in range(N_SLOTS + LAG + 4):
+            for c in range(BIAS_FIRST, N_CHUNKS):
+                if 4 * c + LAG - BIAS_AHEAD == s:
+                    load_bias(c)
             def t_runs():
                 for c in range(1, N_CHUNKS):
                     if tv_slot(c) == s:

@@ -40,8 +40,13 @@ HEAD_V0 = (False, False)
 HEAD_U1 = (False, False)
 QV0_HALVES = True
 BIAS_FIRST = 2
+WQ_BUFS = 8
+SPLIT_LAST = 1
+U0_QUARTERS = True
+EP_BUFS = 10
 BIAS_AHEAD = 6
 TV1_SLOT = 0
+TV2_SLOT = 3
 T_AFTER = False
 
 
@@ -56,8 +61,8 @@ def tile_hybridsuperlayer_pa_kernel(tc, x, c_fc_U, c_fc_S, c_fc_V, c_fc_bias, ou
         keep = ctx.enter_context(tc.tile_pool(name="keep", bufs=1))
         vg_pool = ctx.enter_context(tc.tile_pool(name="vg", bufs=2))
         vq_pool = ctx.enter_context(tc.tile_pool(name="vq", bufs=3))
-        wq_pool = ctx.enter_context(tc.tile_pool(name="wq", bufs=6))
-        ep_pool = ctx.enter_context(tc.tile_pool(name="ep", bufs=6))
+        wq_pool = ctx.enter_context(tc.tile_pool(name="wq", bufs=WQ_BUFS))
+        ep_pool = ctx.enter_context(tc.tile_pool(name="ep", bufs=EP_BUFS))
         psum = ctx.enter_context(tc.psum_pool(name="psum", bufs=8))
         ctx.enter_context(tc.manual_schedule())
 
@@ -81,11 +86,17 @@ def tile_hybridsuperlayer_pa_kernel(tc, x, c_fc_U, c_fc_S, c_fc_V, c_fc_bias, ou
         def load_bias(c):
             nc.sync.dma_start(out=bias_bc[c][:], in_=c_fc_bias[c * CHUNK : (c + 1) * CHUNK].partition_broadcast(P))
 
+        if U0_QUARTERS:
+            for t in range(2):
+                nc.sync.dma_start(out=u_raw[0][:, t : t + 1, :], in_=u_view[0][:, t : t + 1, :])
+            nc.sync.dma_start(out=u_raw[0][:, 2:4, :], in_=u_view[0][:, 2:4, :])
+        else:
+            for h in range(2):
+                nc.sync.dma_start(out=u_raw[0][:, 2 * h : 2 * h + 2, :], in_=u_view[0][:, 2 * h : 2 * h + 2, :])
         nc.sync.dma_start(out=s4[:, 0, :], in_=c_fc_S.rearrange("(p t) -> p t", t=4))
-        for h in range(2):
-            nc.sync.dma_start(out=u_raw[0][:, 2 * h : 2 * h + 2, :], in_=u_view[0][:, 2 * h : 2 * h + 2, :])
         load_v(0)
-        nc.sync.dma_start(out=u_raw[1][:], in_=u_view[1])
+        for h in range(2):
+            nc.sync.dma_start(out=u_raw[1][:, 2 * h : 2 * h + 2, :], in_=u_view[1][:, 2 * h : 2 * h + 2, :])
         load_v(1)
         for i in range(4):
             nc.sync.dma_start(out=x_raw[i][:], in_=x_rows[i * P : (i + 1) * P, :])
@@ -194,32 +205,48 @@ def tile_hybridsuperlayer_pa_kernel(tc, x, c_fc_U, c_fc_S, c_fc_V, c_fc_bias, ou
             dst = w_grouped[(c, g)][:, 4 * HALF * h : 4 * HALF * (h + 1)].rearrange("p (f t) -> p f t", t=4)
             copy_out(on_vector, dst, banks[("w", n)][:].rearrange("p t f -> p f t"))
 
+        def pieces(k):
+            return 2 if k >= N_SLOTS - SPLIT_LAST else 1
+
         def s2(k):
             c, i = k // 4, k % 4
-            acc = psum.tile([P, CHUNK], F32, tag="bank", name="acc")
             toks = slice(i * P, (i + 1) * P)
-            for g in range(2):
-                nc.tensor.matmul_mx(
-                    out=acc[:],
-                    lhsT=x_q[g][0][:, toks].bitcast(FP8X4),
-                    lhsT_scale=x_q[g][1][:, toks],
-                    rhs=w_q[(c, g)][0][:].bitcast(FP8X4),
-                    rhs_scale=w_q[(c, g)][1][:],
-                    start=(g == 0),
-                    stop=(g == 1),
-                )
-            banks[("a", k)] = acc
+            n = pieces(k)
+            width = CHUNK // n
+            for j in range(n):
+                acc = psum.tile([P, width], F32, tag="bank", name="acc")
+                cols = slice(j * width, (j + 1) * width)
+                for g in range(2):
+                    nc.tensor.matmul_mx(
+                        out=acc[:],
+                        lhsT=x_q[g][0][:, toks].bitcast(FP8X4),
+                        lhsT_scale=x_q[g][1][:, toks],
+                        rhs=w_q[(c, g)][0][:, cols].bitcast(FP8X4),
+                        rhs_scale=w_q[(c, g)][1][:, cols],
+                        start=(g == 0),
+                        stop=(g == 1),
+                    )
+                banks[("a", k, j)] = acc
 
         def add(k):
             c = k // 4
-            h_tiles[k] = ep_pool.tile([P, CHUNK], F32, tag="h_sb", name="h_sb")
-            nc.vector.tensor_tensor(out=h_tiles[k][:], in0=banks[("a", k)][:], in1=bias_bc[c][:], op=ALU.add)
+            n = pieces(k)
+            width = CHUNK // n
+            for j in range(n):
+                h_tiles[(k, j)] = ep_pool.tile([P, width], F32, tag="h_sb", name="h_sb")
+                nc.vector.tensor_tensor(
+                    out=h_tiles[(k, j)][:], in0=banks[("a", k, j)][:], in1=bias_bc[c][:, j * width : (j + 1) * width], op=ALU.add
+                )
 
         def gelu(k):
             c, i = k // 4, k % 4
-            o_sb = ep_pool.tile([P, CHUNK], F32, tag="o_sb")
-            nc.scalar.activation(out=o_sb[:], in_=h_tiles[k][:], func=ACT.Gelu)
-            nc.sync.dma_start(out=out_rows[i * P : (i + 1) * P, c * CHUNK : (c + 1) * CHUNK], in_=o_sb[:])
+            n = pieces(k)
+            width = CHUNK // n
+            for j in range(n):
+                o_sb = ep_pool.tile([P, width], F32, tag="o_sb", name="o_sb")
+                nc.scalar.activation(out=o_sb[:], in_=h_tiles[(k, j)][:], func=ACT.Gelu)
+                first = c * CHUNK + j * width
+                nc.sync.dma_start(out=out_rows[i * P : (i + 1) * P, first : first + width], in_=o_sb[:])
 
         def quantize_v0(h):
             if h == 0:
@@ -254,9 +281,9 @@ def tile_hybridsuperlayer_pa_kernel(tc, x, c_fc_U, c_fc_S, c_fc_V, c_fc_bias, ou
         us_q[1] = quantize(us_grouped[1], "us1", keep)
 
         def tv_slot(c):
-            return TV1_SLOT if c == 1 else 4 * c - A_TV
+            return TV1_SLOT if c == 1 else (TV2_SLOT if c == 2 else 4 * c - A_TV)
 
-        for s in range(N_SLOTS + LAG + 4):
+        for s in range(N_SLOTS + LAG + D_G + 2):
             for c in range(BIAS_FIRST, N_CHUNKS):
                 if 4 * c + LAG - BIAS_AHEAD == s:
                     load_bias(c)

@@ -19,18 +19,18 @@ N_CHUNKS = DFF // CHUNK
 FLOPS = 2 * D * DFF * R + 2 * TOKENS * DFF * D
 N_SLOTS = 4 * N_CHUNKS
 
-LAG = 8
-A_TV = 5
+LAG = 9
+A_TV = 4
 D_CW = 1
 D_CV = 0
 D_QV = 2
 D_QW = 2
 D_ADD = 1
 D_G = 2
-X_SLOTS = (1, 2)
-D_CX = 0
-D_QX = 2
-VEC_W = (1,)
+X_SLOTS = (2, 3)
+D_CX = 1
+D_QX = 3
+VEC_W = (3,)
 VEC_V = (1,)
 VEC_X = (0,)
 DVE_ORDER = ("add", "cw", "cv", "cx", "qw", "qv", "qx")
@@ -40,13 +40,16 @@ HEAD_V0 = (False, False)
 HEAD_U1 = (False, False)
 QV0_HALVES = True
 BIAS_FIRST = 2
+GP_BANKS = (3,)
+VEC_V_ODD = (0, 1)
+D_QW1 = 4
 WQ_BUFS = 8
 SPLIT_LAST = 1
 U0_QUARTERS = True
 EP_BUFS = 10
 BIAS_AHEAD = 6
 TV1_SLOT = 0
-TV2_SLOT = 3
+TV2_SLOT = 4
 T_AFTER = False
 
 
@@ -62,6 +65,7 @@ def tile_hybridsuperlayer_pa_kernel(tc, x, c_fc_U, c_fc_S, c_fc_V, c_fc_bias, ou
         vg_pool = ctx.enter_context(tc.tile_pool(name="vg", bufs=2))
         vq_pool = ctx.enter_context(tc.tile_pool(name="vq", bufs=3))
         wq_pool = ctx.enter_context(tc.tile_pool(name="wq", bufs=WQ_BUFS))
+        wf_pool = ctx.enter_context(tc.tile_pool(name="wf", bufs=3))
         ep_pool = ctx.enter_context(tc.tile_pool(name="ep", bufs=EP_BUFS))
         psum = ctx.enter_context(tc.psum_pool(name="psum", bufs=8))
         ctx.enter_context(tc.manual_schedule())
@@ -143,6 +147,7 @@ def tile_hybridsuperlayer_pa_kernel(tc, x, c_fc_U, c_fc_S, c_fc_V, c_fc_bias, ou
         w_q = {}
         h_tiles = {}
         banks = {}
+        w_flat = {}
 
         def scale_u(g, h):
             cols = slice(1024 * h, 1024 * (h + 1))
@@ -203,7 +208,18 @@ def tile_hybridsuperlayer_pa_kernel(tc, x, c_fc_U, c_fc_S, c_fc_V, c_fc_bias, ou
             if h == 0:
                 w_grouped[(c, g)] = wq_pool.tile([P, 4 * CHUNK], BF16, tag="w_grouped", name="w_grouped", align_bytes=64)
             dst = w_grouped[(c, g)][:, 4 * HALF * h : 4 * HALF * (h + 1)].rearrange("p (f t) -> p f t", t=4)
-            copy_out(on_vector, dst, banks[("w", n)][:].rearrange("p t f -> p f t"))
+            if n % 4 in GP_BANKS:
+                w_flat[n] = wf_pool.tile([P, 4, HALF], BF16, tag="w_flat", name="w_flat")
+                copy_out(on_vector, w_flat[n][:], banks[("w", n)][:])
+            else:
+                copy_out(on_vector, dst, banks[("w", n)][:].rearrange("p t f -> p f t"))
+
+        def gi(n):
+            c, g, h = n // 4, (n % 4) // 2, n % 2
+            dst = w_grouped[(c, g)][:, 4 * HALF * h : 4 * HALF * (h + 1)].rearrange("p (f t) -> p f t", t=4)
+            nc.gpsimd.tensor_scalar(
+                out=dst, in0=w_flat[n][:].rearrange("p t f -> p f t"), scalar1=1.0, scalar2=0.0, op0=ALU.mult, op1=ALU.add
+            )
 
         def pieces(k):
             return 2 if k >= N_SLOTS - SPLIT_LAST else 1
@@ -310,7 +326,7 @@ def tile_hybridsuperlayer_pa_kernel(tc, x, c_fc_U, c_fc_S, c_fc_V, c_fc_bias, ou
                 if what == "cv":
                     for c in range(1, N_CHUNKS):
                         if tv_slot(c) + D_CV == s:
-                            for h in VEC_V:
+                            for h in (VEC_V_ODD if c % 2 else VEC_V):
                                 cv(c, h, True)
                 if what == "cx":
                     for g in range(2):
@@ -326,7 +342,7 @@ def tile_hybridsuperlayer_pa_kernel(tc, x, c_fc_U, c_fc_S, c_fc_V, c_fc_bias, ou
                     for c in range(1, N_CHUNKS):
                         if tv_slot(c) + D_CV == s:
                             for h in range(2):
-                                if h not in VEC_V:
+                                if h not in (VEC_V_ODD if c % 2 else VEC_V):
                                     cv(c, h, False)
                 if what == "cx":
                     for g in range(2):
@@ -334,11 +350,13 @@ def tile_hybridsuperlayer_pa_kernel(tc, x, c_fc_U, c_fc_S, c_fc_V, c_fc_bias, ou
                             for h in range(2):
                                 if h not in VEC_X:
                                     cx(g, h, False)
+            if 0 <= s - D_CW < N_SLOTS and (s - D_CW) % 4 in GP_BANKS:
+                gi(s - D_CW)
             for what in DVE_ORDER:
                 if what == "qw":
                     for c in range(N_CHUNKS):
                         for g in range(2):
-                            if 4 * c + 2 * g + 1 + D_QW == s:
+                            if 4 * c + 2 * g + 1 + (D_QW, D_QW1)[g] == s:
                                 w_q[(c, g)] = quantize(w_grouped[(c, g)], "w", wq_pool)
                 if what == "qv":
                     for c in range(1, N_CHUNKS):

@@ -58,7 +58,10 @@ def tile_hybridsuperlayer_pa_kernel(tc, x, c_fc_U, c_fc_S, c_fc_V, c_fc_bias, ou
     x_rows = x.flatten_outer_dims()
     out_rows = out.flatten_outer_dims()
     u_view = c_fc_U.rearrange("(g m t) r -> g m t r", g=2, t=4)
-    v_view = c_fc_V.rearrange("(c h p j) r -> c h p j r", c=N_CHUNKS, h=2, j=2)
+    v_halves = c_fc_V.rearrange("(c h p j) r -> c h p j r", c=N_CHUNKS, h=2, j=2)
+    v_view = c_fc_V.rearrange("(c p j) r -> c p j r", c=N_CHUNKS, j=4)
+    x_view = x_rows.rearrange("(p j) d -> p j d", j=4)
+    out_view = out_rows.rearrange("(p j) f -> j p f", j=4)
 
     with ExitStack() as ctx:
         keep = ctx.enter_context(tc.tile_pool(name="keep", bufs=1))
@@ -79,13 +82,16 @@ def tile_hybridsuperlayer_pa_kernel(tc, x, c_fc_U, c_fc_S, c_fc_V, c_fc_bias, ou
 
         s4 = keep.tile([P, 1, 4], BF16)
         u_raw = [keep.tile([P, 4, R], BF16, name="u_raw%d" % g) for g in range(2)]
-        v_raw = [keep.tile([P, 2, 2, R], BF16, name="v_raw%d" % c) for c in range(N_CHUNKS)]
-        x_raw = [keep.tile([P, D], BF16, name="x_raw%d" % i) for i in range(4)]
+        v_raw = [keep.tile([P, 4, R], BF16, name="v_raw%d" % c) for c in range(N_CHUNKS)]
+        x_raw = keep.tile([P, 4, D], BF16)
         bias_bc = [keep.tile([P, CHUNK], BF16, name="bias_bc%d" % c) for c in range(N_CHUNKS)]
 
         def load_v(c):
-            for h in range(2):
-                nc.sync.dma_start(out=v_raw[c][:, h, :, :], in_=v_view[c][h])
+            if c == 0:
+                for h in range(2):
+                    nc.sync.dma_start(out=v_raw[c][:, 2 * h : 2 * h + 2, :], in_=v_halves[c][h])
+            else:
+                nc.sync.dma_start(out=v_raw[c][:], in_=v_view[c])
 
         def load_bias(c):
             nc.sync.dma_start(out=bias_bc[c][:], in_=c_fc_bias[c * CHUNK : (c + 1) * CHUNK].partition_broadcast(P))
@@ -99,11 +105,10 @@ def tile_hybridsuperlayer_pa_kernel(tc, x, c_fc_U, c_fc_S, c_fc_V, c_fc_bias, ou
                 nc.sync.dma_start(out=u_raw[0][:, 2 * h : 2 * h + 2, :], in_=u_view[0][:, 2 * h : 2 * h + 2, :])
         nc.sync.dma_start(out=s4[:, 0, :], in_=c_fc_S.rearrange("(p t) -> p t", t=4))
         load_v(0)
-        for h in range(2):
-            nc.sync.dma_start(out=u_raw[1][:, 2 * h : 2 * h + 2, :], in_=u_view[1][:, 2 * h : 2 * h + 2, :])
+        nc.sync.dma_start(out=u_raw[1][:], in_=u_view[1])
         load_v(1)
-        for i in range(4):
-            nc.sync.dma_start(out=x_raw[i][:], in_=x_rows[i * P : (i + 1) * P, :])
+        for h in range(2):
+            nc.sync.dma_start(out=x_raw[:, 2 * h : 2 * h + 2, :], in_=x_view[:, 2 * h : 2 * h + 2, :])
         load_v(2)
         load_v(3)
         load_v(4)
@@ -170,7 +175,7 @@ def tile_hybridsuperlayer_pa_kernel(tc, x, c_fc_U, c_fc_S, c_fc_V, c_fc_bias, ou
 
         def tx(g):
             for h in range(2):
-                banks[("x", g, h)] = transpose_bank([every_2nd_word(x_raw[2 * h + s][:], 256 * g) for s in range(2)])
+                banks[("x", g, h)] = transpose_bank([every_2nd_word(x_raw[:, 2 * h + s, :], 256 * g) for s in range(2)])
 
         def cx(g, h, on_vector):
             copy_out(on_vector, grouped_half(x_grouped[g], h), banks[("x", g, h)][:].rearrange("p s u m -> p s m u"))
@@ -178,10 +183,13 @@ def tile_hybridsuperlayer_pa_kernel(tc, x, c_fc_U, c_fc_S, c_fc_V, c_fc_bias, ou
         def tv(c):
             v_grouped[c] = vg_pool.tile([P, 4 * CHUNK], BF16, tag="v_grouped", name="v_grouped", align_bytes=64)
             for h in range(2):
-                banks[("v", c, h)] = transpose_bank([every_2nd_word(v_raw[c][:, h, j, :], 0) for j in range(2)])
+                banks[("v", c, h)] = transpose_bank([every_2nd_word(v_raw[c][:, 2 * h + j, :], 0) for j in range(2)])
 
         def cv(c, h, on_vector):
-            dst = v_grouped[c][:, 1024 * h : 1024 * (h + 1)].bitcast(F32).rearrange("k (p j u) -> k p j u", j=2, u=2)
+            if c == 0:
+                dst = v_grouped[c][:, 1024 * h : 1024 * (h + 1)].bitcast(F32).rearrange("k (p j u) -> k p j u", j=2, u=2)
+            else:
+                dst = v_grouped[c][:].bitcast(F32).rearrange("k (p j u) -> k p j u", j=4, u=2)[:, :, 2 * h : 2 * h + 2, :]
             copy_out(on_vector, dst, banks[("v", c, h)][:].rearrange("k j u p -> k p j u"))
 
         def s1(n):
@@ -262,7 +270,7 @@ def tile_hybridsuperlayer_pa_kernel(tc, x, c_fc_U, c_fc_S, c_fc_V, c_fc_bias, ou
                 o_sb = ep_pool.tile([P, width], F32, tag="o_sb", name="o_sb")
                 nc.scalar.activation(out=o_sb[:], in_=h_tiles[(k, j)][:], func=ACT.Gelu)
                 first = c * CHUNK + j * width
-                nc.sync.dma_start(out=out_rows[i * P : (i + 1) * P, first : first + width], in_=o_sb[:])
+                nc.sync.dma_start(out=out_view[i][:, first : first + width], in_=o_sb[:])
 
         def quantize_v0(h):
             if h == 0:

@@ -47,7 +47,7 @@ WQ_BUFS = 8
 SPLIT_LAST = 1
 U0_QUARTERS = True
 EP_BUFS = 10
-BIAS_AHEAD = 6
+BIAS_AHEAD = 14
 TV1_SLOT = 0
 TV2_SLOT = 4
 T_AFTER = False

@@ -46,11 +46,12 @@ D_QW1 = 4
 WQ_BUFS = 8
 SPLIT_LAST = 1
 U0_QUARTERS = True
-EP_BUFS = 10
+EP_BUFS = 7
 BIAS_AHEAD = 14
 TV1_SLOT = 0
 TV2_SLOT = 4
 T_AFTER = False
+SINGLES = 12
 
 
 def tile_hybridsuperlayer_pa_kernel(tc, x, c_fc_U, c_fc_S, c_fc_V, c_fc_bias, out):
@@ -252,8 +253,18 @@ def tile_hybridsuperlayer_pa_kernel(tc, x, c_fc_U, c_fc_S, c_fc_V, c_fc_bias, ou
                     )
                 banks[("a", k, j)] = acc
 
+        out_pairs = out_rows.rearrange("(p j) f -> p j f", j=4)
+
+        def paired(k):
+            return k < N_SLOTS - SINGLES
+
         def add(k):
             c = k // 4
+            if paired(k):
+                if k % 2 == 0:
+                    h_tiles[k // 2] = ep_pool.tile([P, 2, CHUNK], F32, tag="h_sb", name="h_sb")
+                nc.vector.tensor_tensor(out=h_tiles[k // 2][:, k % 2, :], in0=banks[("a", k, 0)][:], in1=bias_bc[c][:], op=ALU.add)
+                return
             n = pieces(k)
             width = CHUNK // n
             for j in range(n):
@@ -264,6 +275,12 @@ def tile_hybridsuperlayer_pa_kernel(tc, x, c_fc_U, c_fc_S, c_fc_V, c_fc_bias, ou
 
         def gelu(k):
             c, i = k // 4, k % 4
+            if paired(k):
+                if k % 2 == 1:
+                    o_pair = ep_pool.tile([P, 2, CHUNK], F32, tag="o_sb", name="o_sb")
+                    nc.scalar.activation(out=o_pair[:], in_=h_tiles[k // 2][:], func=ACT.Gelu)
+                    nc.sync.dma_start(out=out_pairs[:, i - 1 : i + 1, c * CHUNK : (c + 1) * CHUNK], in_=o_pair[:])
+                return
             n = pieces(k)
             width = CHUNK // n
             for j in range(n):

@@ -19,19 +19,20 @@ N_CHUNKS = DFF // CHUNK
 FLOPS = 2 * D * DFF * R + 2 * TOKENS * DFF * D
 N_SLOTS = 4 * N_CHUNKS
 
+LAGS = (9,) * 8
 LAG = 9
 A_TV = 4
 D_CW = 1
 D_CV = 0
 D_QV = 2
-D_QW = 2
+QW_SLOTS = ((3, 7), (3, 7), (3, 7), (3, 7), (3, 7), (3, 7), (3, 7), (3, 7))
 D_ADD = 1
 D_G = 2
 X_SLOTS = (2, 3)
 D_CX = 1
-D_QX = 3
-VEC_W = (3,)
-VEC_V = (1,)
+QX_SLOTS = (5, 6)
+VEC_W = ((3,), (3,), (3,), (3,), (3,), (3,), (3,), (3,))
+VEC_V = ((), (0, 1), (1,), (0, 1), (1,), (0, 1), (1,), (0, 1))
 VEC_X = (0,)
 DVE_ORDER = ("add", "cw", "cv", "cx", "qw", "qv", "qx")
 ACT_ORDER = ("cw", "cv", "cx", "gelu")
@@ -40,9 +41,7 @@ HEAD_V0 = (False, False)
 HEAD_U1 = (False, False)
 QV0_HALVES = True
 BIAS_FIRST = 2
-GP_BANKS = (3,)
-VEC_V_ODD = (0, 1)
-D_QW1 = 4
+GP_BANKS = ((3,), (3,), (3,), (3,), (3,), (3,), (2, 3), (3,))
 WQ_BUFS = 8
 SPLIT_LAST = 1
 U0_QUARTERS = True
@@ -217,7 +216,7 @@ def tile_hybridsuperlayer_pa_kernel(tc, x, c_fc_U, c_fc_S, c_fc_V, c_fc_bias, ou
             if h == 0:
                 w_grouped[(c, g)] = wq_pool.tile([P, 4 * CHUNK], BF16, tag="w_grouped", name="w_grouped", align_bytes=64)
             dst = w_grouped[(c, g)][:, 4 * HALF * h : 4 * HALF * (h + 1)].rearrange("p (f t) -> p f t", t=4)
-            if n % 4 in GP_BANKS:
+            if n % 4 in GP_BANKS[c]:
                 w_flat[n] = wf_pool.tile([P, 4, HALF], BF16, tag="w_flat", name="w_flat")
                 copy_out(on_vector, w_flat[n][:], banks[("w", n)][:])
             else:
@@ -324,6 +323,9 @@ def tile_hybridsuperlayer_pa_kernel(tc, x, c_fc_U, c_fc_S, c_fc_V, c_fc_bias, ou
         def tv_slot(c):
             return TV1_SLOT if c == 1 else (TV2_SLOT if c == 2 else 4 * c - A_TV)
 
+        def tiles_at(slot):
+            return [k for k in range(N_SLOTS) if k + LAGS[k // 4] == slot]
+
         for s in range(N_SLOTS + LAG + D_G + 2):
             for c in range(BIAS_FIRST, N_CHUNKS):
                 if 4 * c + LAG - BIAS_AHEAD == s:
@@ -339,19 +341,20 @@ def tile_hybridsuperlayer_pa_kernel(tc, x, c_fc_U, c_fc_S, c_fc_V, c_fc_bias, ou
                 t_runs()
             if s < N_SLOTS:
                 s1(s)
-            if 0 <= s - LAG < N_SLOTS:
-                s2(s - LAG)
+            for k in tiles_at(s):
+                s2(k)
             if T_AFTER:
                 t_runs()
             for what in DVE_ORDER:
-                if what == "add" and 0 <= s - LAG - D_ADD < N_SLOTS:
-                    add(s - LAG - D_ADD)
-                if what == "cw" and 0 <= s - D_CW < N_SLOTS and (s - D_CW) % 4 in VEC_W:
+                if what == "add":
+                    for k in tiles_at(s - D_ADD):
+                        add(k)
+                if what == "cw" and 0 <= s - D_CW < N_SLOTS and (s - D_CW) % 4 in VEC_W[(s - D_CW) // 4]:
                     cw(s - D_CW, True)
                 if what == "cv":
                     for c in range(1, N_CHUNKS):
                         if tv_slot(c) + D_CV == s:
-                            for h in (VEC_V_ODD if c % 2 else VEC_V):
+                            for h in VEC_V[c]:
                                 cv(c, h, True)
                 if what == "cx":
                     for g in range(2):
@@ -359,15 +362,16 @@ def tile_hybridsuperlayer_pa_kernel(tc, x, c_fc_U, c_fc_S, c_fc_V, c_fc_bias, ou
                             for h in VEC_X:
                                 cx(g, h, True)
             for what in ACT_ORDER:
-                if what == "gelu" and 0 <= s - LAG - D_G < N_SLOTS:
-                    gelu(s - LAG - D_G)
-                if what == "cw" and 0 <= s - D_CW < N_SLOTS and (s - D_CW) % 4 not in VEC_W:
+                if what == "gelu":
+                    for k in tiles_at(s - D_G):
+                        gelu(k)
+                if what == "cw" and 0 <= s - D_CW < N_SLOTS and (s - D_CW) % 4 not in VEC_W[(s - D_CW) // 4]:
                     cw(s - D_CW, False)
                 if what == "cv":
                     for c in range(1, N_CHUNKS):
                         if tv_slot(c) + D_CV == s:
                             for h in range(2):
-                                if h not in (VEC_V_ODD if c % 2 else VEC_V):
+                                if h not in VEC_V[c]:
                                     cv(c, h, False)
                 if what == "cx":
                     for g in range(2):
@@ -375,13 +379,13 @@ def tile_hybridsuperlayer_pa_kernel(tc, x, c_fc_U, c_fc_S, c_fc_V, c_fc_bias, ou
                             for h in range(2):
                                 if h not in VEC_X:
                                     cx(g, h, False)
-            if 0 <= s - D_CW < N_SLOTS and (s - D_CW) % 4 in GP_BANKS:
+            if 0 <= s - D_CW < N_SLOTS and (s - D_CW) % 4 in GP_BANKS[(s - D_CW) // 4]:
                 gi(s - D_CW)
             for what in DVE_ORDER:
                 if what == "qw":
                     for c in range(N_CHUNKS):
                         for g in range(2):
-                            if 4 * c + 2 * g + 1 + (D_QW, D_QW1)[g] == s:
+                            if 4 * c + QW_SLOTS[c][g] == s:
                                 w_q[(c, g)] = quantize(w_grouped[(c, g)], "w", wq_pool)
                 if what == "qv":
                     for c in range(1, N_CHUNKS):
@@ -389,5 +393,5 @@ def tile_hybridsuperlayer_pa_kernel(tc, x, c_fc_U, c_fc_S, c_fc_V, c_fc_bias, ou
                             v_q[c] = quantize(v_grouped[c], "v", vq_pool)
                 if what == "qx":
                     for g in range(2):
-                        if X_SLOTS[g] + D_QX == s:
+                        if QX_SLOTS[g] == s:
                             x_q[g] = quantize(x_grouped[g], "x%d" % g, keep)

@@ -34,8 +34,18 @@ QX_SLOTS = (5, 6)
 VEC_W = ((3,), (3,), (3,), (3,), (3,), (3,), (3,), (3,))
 VEC_V = ((), (0, 1), (1,), (0, 1), (1,), (0, 1), (1,), (0, 1))
 VEC_X = (0,)
-DVE_ORDER = ("add", "cw", "cv", "cx", "qw", "qv", "qx")
-ACT_ORDER = ("cw", "cv", "cx", "gelu")
+DVE_ORDERS = (("cw", "add", "cv", "cx", "ord", "|", "qw", "qv", "qx"),) * 4
+W1_BUFS = 0
+ORD_V = {}
+FUSE_U = False
+QW_REV = False
+U0_ONE = False
+V0_ONE = False
+VI_BANKS = ((),) * 8
+STORE_SINGLES = 12
+WARM = {}
+ORD_X = {}
+ACT_ORDER = ("cw", "cv", "cx", "ord", "gelu")
 HEAD_U0 = (False, False)
 HEAD_V0 = (False, False)
 HEAD_U1 = (False, False)
@@ -68,6 +78,8 @@ def tile_hybridsuperlayer_pa_kernel(tc, x, c_fc_U, c_fc_S, c_fc_V, c_fc_bias, ou
         vg_pool = ctx.enter_context(tc.tile_pool(name="vg", bufs=2))
         vq_pool = ctx.enter_context(tc.tile_pool(name="vq", bufs=3))
         wq_pool = ctx.enter_context(tc.tile_pool(name="wq", bufs=WQ_BUFS))
+        w1_pool = ctx.enter_context(tc.tile_pool(name="w1", bufs=W1_BUFS)) if W1_BUFS else wq_pool
+        ord_pool = ctx.enter_context(tc.tile_pool(name="ord", bufs=2)) if (ORD_V or ORD_X) else keep
         wf_pool = ctx.enter_context(tc.tile_pool(name="wf", bufs=3))
         ep_pool = ctx.enter_context(tc.tile_pool(name="ep", bufs=EP_BUFS))
         psum = ctx.enter_context(tc.psum_pool(name="psum", bufs=8))
@@ -78,6 +90,9 @@ def tile_hybridsuperlayer_pa_kernel(tc, x, c_fc_U, c_fc_S, c_fc_V, c_fc_bias, ou
         warm_in = keep.tile([P, 1], F32)
         warm_out = keep.tile([P, 1], F32)
         nc.vector.memset(warm_in[:], 0.0)
+        zeros = keep.tile([P, CHUNK], BF16, name="zeros") if WARM else None
+        if WARM:
+            nc.vector.memset(zeros[:], 0.0)
         nc.scalar.activation(out=warm_out[:], in_=warm_in[:], func=ACT.Gelu)
 
         s4 = keep.tile([P, 1, 4], BF16)
@@ -87,7 +102,7 @@ def tile_hybridsuperlayer_pa_kernel(tc, x, c_fc_U, c_fc_S, c_fc_V, c_fc_bias, ou
         bias_bc = [keep.tile([P, CHUNK], BF16, name="bias_bc%d" % c) for c in range(N_CHUNKS)]
 
         def load_v(c):
-            if c == 0:
+            if c == 0 and not V0_ONE:
                 for h in range(2):
                     nc.sync.dma_start(out=v_raw[c][:, 2 * h : 2 * h + 2, :], in_=v_halves[c][h])
             else:
@@ -96,7 +111,9 @@ def tile_hybridsuperlayer_pa_kernel(tc, x, c_fc_U, c_fc_S, c_fc_V, c_fc_bias, ou
         def load_bias(c):
             nc.sync.dma_start(out=bias_bc[c][:], in_=c_fc_bias[c * CHUNK : (c + 1) * CHUNK].partition_broadcast(P))
 
-        if U0_QUARTERS:
+        if U0_ONE:
+            nc.sync.dma_start(out=u_raw[0][:], in_=u_view[0])
+        elif U0_QUARTERS:
             for t in range(2):
                 nc.sync.dma_start(out=u_raw[0][:, t : t + 1, :], in_=u_view[0][:, t : t + 1, :])
             nc.sync.dma_start(out=u_raw[0][:, 2:4, :], in_=u_view[0][:, 2:4, :])
@@ -124,8 +141,10 @@ def tile_hybridsuperlayer_pa_kernel(tc, x, c_fc_U, c_fc_S, c_fc_V, c_fc_bias, ou
             else:
                 nc.scalar.copy(out=dst, in_=src)
 
-        def transpose_bank(words):
+        def transpose_bank(words, warm_passes=0):
             bank = psum.tile([P, 2, 2, P], F32, tag="bank", name="tp_bank")
+            for i in range(warm_passes):
+                nc.tensor.matmul(out=bank[:].rearrange("p s u m -> p (s u m)"), lhsT=zeros[:, 0:P], rhs=zeros[:], start=True, stop=True)
             for s in range(2):
                 for u in range(2):
                     nc.tensor.transpose(bank[:, s, u, :], words[s][u], ident[:])
@@ -153,6 +172,9 @@ def tile_hybridsuperlayer_pa_kernel(tc, x, c_fc_U, c_fc_S, c_fc_V, c_fc_bias, ou
         h_tiles = {}
         banks = {}
         w_flat = {}
+        x_ord = {}
+        o_pairs = {}
+        v_ord = {}
 
         def scale_u(g, h):
             cols = slice(1024 * h, 1024 * (h + 1))
@@ -168,14 +190,38 @@ def tile_hybridsuperlayer_pa_kernel(tc, x, c_fc_U, c_fc_S, c_fc_V, c_fc_bias, ou
 
         def tu(g):
             for h in range(2):
-                banks[("u", g, h)] = transpose_bank([every_2nd_word(u_raw[g][:, 2 * h + s, :], 0) for s in range(2)])
+                banks[("u", g, h)] = transpose_bank([every_2nd_word(u_raw[g][:, 2 * h + s, :], 0) for s in range(2)], WARM.get(("u", g, h), 0))
 
         def cu(g, h, on_vector):
             copy_out(on_vector, grouped_half(u_grouped[g], h), banks[("u", g, h)][:].rearrange("p s u m -> p s m u"))
 
+        def order_words(on_vector, dst, src):
+            copy_out(on_vector, dst[:], src.bitcast(F32).rearrange("p j (m u) -> p j u m", u=2))
+
+        def ox(g, on_vector):
+            x_ord[g] = ord_pool.tile([P, 4, 2, P], F32, tag="x_ord", name="x_ord")
+            order_words(on_vector, x_ord[g], x_raw[:, :, 512 * g : 512 * (g + 1)])
+
+        def ov(c, on_vector):
+            v_ord[c] = ord_pool.tile([P, 4, 2, P], F32, tag="v_ord", name="v_ord")
+            order_words(on_vector, v_ord[c], v_raw[c][:])
+
+        def cus(g, h):
+            for s in range(2):
+                first = 1024 * h + 512 * s
+                nc.vector.tensor_tensor(
+                    out=us_grouped[g][:, first : first + 512].rearrange("p (m u e) -> p m u e", u=2, e=2),
+                    in0=banks[("u", g, h)][:, s, :, :].bitcast(BF16).rearrange("p u (m e) -> p m u e", e=2),
+                    in1=s4[:].rearrange("p o (u e) -> p o u e", u=2).to_broadcast([P, P, 2, 2]),
+                    op=ALU.mult,
+                )
+
         def tx(g):
             for h in range(2):
-                banks[("x", g, h)] = transpose_bank([every_2nd_word(x_raw[:, 2 * h + s, :], 256 * g) for s in range(2)])
+                if g in ORD_X:
+                    banks[("x", g, h)] = transpose_bank([[x_ord[g][:, 2 * h + s, u, :] for u in range(2)] for s in range(2)])
+                else:
+                    banks[("x", g, h)] = transpose_bank([every_2nd_word(x_raw[:, 2 * h + s, :], 256 * g) for s in range(2)])
 
         def cx(g, h, on_vector):
             copy_out(on_vector, grouped_half(x_grouped[g], h), banks[("x", g, h)][:].rearrange("p s u m -> p s m u"))
@@ -183,10 +229,13 @@ def tile_hybridsuperlayer_pa_kernel(tc, x, c_fc_U, c_fc_S, c_fc_V, c_fc_bias, ou
         def tv(c):
             v_grouped[c] = vg_pool.tile([P, 4 * CHUNK], BF16, tag="v_grouped", name="v_grouped", align_bytes=64)
             for h in range(2):
-                banks[("v", c, h)] = transpose_bank([every_2nd_word(v_raw[c][:, 2 * h + j, :], 0) for j in range(2)])
+                if c in ORD_V:
+                    banks[("v", c, h)] = transpose_bank([[v_ord[c][:, 2 * h + j, u, :] for u in range(2)] for j in range(2)])
+                else:
+                    banks[("v", c, h)] = transpose_bank([every_2nd_word(v_raw[c][:, 2 * h + j, :], 0) for j in range(2)], WARM.get(("v", c, h), 0))
 
         def cv(c, h, on_vector):
-            if c == 0:
+            if c == 0 and not V0_ONE:
                 dst = v_grouped[c][:, 1024 * h : 1024 * (h + 1)].bitcast(F32).rearrange("k (p j u) -> k p j u", j=2, u=2)
             else:
                 dst = v_grouped[c][:].bitcast(F32).rearrange("k (p j u) -> k p j u", j=4, u=2)[:, :, 2 * h : 2 * h + 2, :]
@@ -214,7 +263,7 @@ def tile_hybridsuperlayer_pa_kernel(tc, x, c_fc_U, c_fc_S, c_fc_V, c_fc_bias, ou
         def cw(n, on_vector):
             c, g, h = n // 4, (n % 4) // 2, n % 2
             if h == 0:
-                w_grouped[(c, g)] = wq_pool.tile([P, 4 * CHUNK], BF16, tag="w_grouped", name="w_grouped", align_bytes=64)
+                w_grouped[(c, g)] = (wq_pool, w1_pool)[g].tile([P, 4 * CHUNK], BF16, tag="w_grouped", name="w_grouped", align_bytes=64)
             dst = w_grouped[(c, g)][:, 4 * HALF * h : 4 * HALF * (h + 1)].rearrange("p (f t) -> p f t", t=4)
             if n % 4 in GP_BANKS[c]:
                 w_flat[n] = wf_pool.tile([P, 4, HALF], BF16, tag="w_flat", name="w_flat")
@@ -225,9 +274,12 @@ def tile_hybridsuperlayer_pa_kernel(tc, x, c_fc_U, c_fc_S, c_fc_V, c_fc_bias, ou
         def gi(n):
             c, g, h = n // 4, (n % 4) // 2, n % 2
             dst = w_grouped[(c, g)][:, 4 * HALF * h : 4 * HALF * (h + 1)].rearrange("p (f t) -> p f t", t=4)
-            nc.gpsimd.tensor_scalar(
-                out=dst, in0=w_flat[n][:].rearrange("p t f -> p f t"), scalar1=1.0, scalar2=0.0, op0=ALU.mult, op1=ALU.add
-            )
+            if n % 4 in VI_BANKS[c]:
+                nc.vector.tensor_copy(out=dst, in_=w_flat[n][:].rearrange("p t f -> p f t"))
+            else:
+                nc.gpsimd.tensor_scalar(
+                    out=dst, in0=w_flat[n][:].rearrange("p t f -> p f t"), scalar1=1.0, scalar2=0.0, op0=ALU.mult, op1=ALU.add
+                )
 
         def pieces(k):
             return 2 if k >= N_SLOTS - SPLIT_LAST else 1
@@ -280,6 +332,13 @@ def tile_hybridsuperlayer_pa_kernel(tc, x, c_fc_U, c_fc_S, c_fc_V, c_fc_bias, ou
                     nc.scalar.activation(out=o_pair[:], in_=h_tiles[k // 2][:], func=ACT.Gelu)
                     nc.sync.dma_start(out=out_pairs[:, i - 1 : i + 1, c * CHUNK : (c + 1) * CHUNK], in_=o_pair[:])
                 return
+            if k < N_SLOTS - STORE_SINGLES:
+                if k % 2 == 0:
+                    o_pairs[k // 2] = ep_pool.tile([P, 2, CHUNK], F32, tag="o_sb", name="o_sb")
+                nc.scalar.activation(out=o_pairs[k // 2][:, k % 2, :], in_=h_tiles[(k, 0)][:], func=ACT.Gelu)
+                if k % 2 == 1:
+                    nc.sync.dma_start(out=out_pairs[:, i - 1 : i + 1, c * CHUNK : (c + 1) * CHUNK], in_=o_pairs[k // 2][:])
+                return
             n = pieces(k)
             width = CHUNK // n
             for j in range(n):
@@ -300,10 +359,14 @@ def tile_hybridsuperlayer_pa_kernel(tc, x, c_fc_U, c_fc_S, c_fc_V, c_fc_bias, ou
             )
 
         tu(0)
-        cu(0, 0, HEAD_U0[0])
-        cu(0, 1, HEAD_U0[1])
-        scale_u(0, 0)
-        scale_u(0, 1)
+        if FUSE_U:
+            cus(0, 0)
+            cus(0, 1)
+        else:
+            cu(0, 0, HEAD_U0[0])
+            cu(0, 1, HEAD_U0[1])
+            scale_u(0, 0)
+            scale_u(0, 1)
         tv(0)
         cv(0, 0, HEAD_V0[0])
         cv(0, 1, HEAD_V0[1])
@@ -314,10 +377,14 @@ def tile_hybridsuperlayer_pa_kernel(tc, x, c_fc_U, c_fc_S, c_fc_V, c_fc_bias, ou
         else:
             v_q[0] = quantize(v_grouped[0], "v", vq_pool)
         tu(1)
-        cu(1, 0, HEAD_U1[0])
-        cu(1, 1, HEAD_U1[1])
-        scale_u(1, 0)
-        scale_u(1, 1)
+        if FUSE_U:
+            cus(1, 0)
+            cus(1, 1)
+        else:
+            cu(1, 0, HEAD_U1[0])
+            cu(1, 1, HEAD_U1[1])
+            scale_u(1, 0)
+            scale_u(1, 1)
         us_q[1] = quantize(us_grouped[1], "us1", keep)
 
         def tv_slot(c):
@@ -325,6 +392,44 @@ def tile_hybridsuperlayer_pa_kernel(tc, x, c_fc_U, c_fc_S, c_fc_V, c_fc_bias, ou
 
         def tiles_at(slot):
             return [k for k in range(N_SLOTS) if k + LAGS[k // 4] == slot]
+
+        def vector_part(s, kinds):
+            for what in kinds:
+                if what == "ord":
+                    for g in sorted(ORD_X):
+                        if ORD_X[g] == (s, True):
+                            ox(g, True)
+                    for c in sorted(ORD_V):
+                        if ORD_V[c] == (s, True):
+                            ov(c, True)
+                if what == "add":
+                    for k in tiles_at(s - D_ADD):
+                        add(k)
+                if what == "cw" and 0 <= s - D_CW < N_SLOTS and (s - D_CW) % 4 in VEC_W[(s - D_CW) // 4]:
+                    cw(s - D_CW, True)
+                if what == "cv":
+                    for c in range(1, N_CHUNKS):
+                        if tv_slot(c) + D_CV == s:
+                            for h in VEC_V[c]:
+                                cv(c, h, True)
+                if what == "cx":
+                    for g in range(2):
+                        if X_SLOTS[g] + D_CX == s:
+                            for h in VEC_X:
+                                cx(g, h, True)
+                if what == "qw":
+                    for c in (list(reversed(range(N_CHUNKS))) if QW_REV else list(range(N_CHUNKS))):
+                        for g in range(2):
+                            if 4 * c + QW_SLOTS[c][g] == s:
+                                w_q[(c, g)] = quantize(w_grouped[(c, g)], "w", wq_pool)
+                if what == "qv":
+                    for c in range(1, N_CHUNKS):
+                        if tv_slot(c) + D_QV == s:
+                            v_q[c] = quantize(v_grouped[c], "v", vq_pool)
+                if what == "qx":
+                    for g in range(2):
+                        if QX_SLOTS[g] == s:
+                            x_q[g] = quantize(x_grouped[g], "x%d" % g, keep)
 
         for s in range(N_SLOTS + LAG + D_G + 2):
             for c in range(BIAS_FIRST, N_CHUNKS):
@@ -345,23 +450,16 @@ def tile_hybridsuperlayer_pa_kernel(tc, x, c_fc_U, c_fc_S, c_fc_V, c_fc_bias, ou
                 s2(k)
             if T_AFTER:
                 t_runs()
-            for what in DVE_ORDER:
-                if what == "add":
-                    for k in tiles_at(s - D_ADD):
-                        add(k)
-                if what == "cw" and 0 <= s - D_CW < N_SLOTS and (s - D_CW) % 4 in VEC_W[(s - D_CW) // 4]:
-                    cw(s - D_CW, True)
-                if what == "cv":
-                    for c in range(1, N_CHUNKS):
-                        if tv_slot(c) + D_CV == s:
-                            for h in VEC_V[c]:
-                                cv(c, h, True)
-                if what == "cx":
-                    for g in range(2):
-                        if X_SLOTS[g] + D_CX == s:
-                            for h in VEC_X:
-                                cx(g, h, True)
+            order = DVE_ORDERS[s % 4]
+            vector_part(s, order[: order.index("|")])
             for what in ACT_ORDER:
+                if what == "ord":
+                    for g in sorted(ORD_X):
+                        if ORD_X[g] == (s, False):
+                            ox(g, False)
+                    for c in sorted(ORD_V):
+                        if ORD_V[c] == (s, False):
+                            ov(c, False)
                 if what == "gelu":
                     for k in tiles_at(s - D_G):
                         gelu(k)
@@ -381,17 +479,4 @@ def tile_hybridsuperlayer_pa_kernel(tc, x, c_fc_U, c_fc_S, c_fc_V, c_fc_bias, ou
                                     cx(g, h, False)
             if 0 <= s - D_CW < N_SLOTS and (s - D_CW) % 4 in GP_BANKS[(s - D_CW) // 4]:
                 gi(s - D_CW)
-            for what in DVE_ORDER:
-                if what == "qw":
-                    for c in range(N_CHUNKS):
-                        for g in range(2):
-                            if 4 * c + QW_SLOTS[c][g] == s:
-                                w_q[(c, g)] = quantize(w_grouped[(c, g)], "w", wq_pool)
-                if what == "qv":
-                    for c in range(1, N_CHUNKS):
-                        if tv_slot(c) + D_QV == s:
-                            v_q[c] = quantize(v_grouped[c], "v", vq_pool)
-                if what == "qx":
-                    for g in range(2):
-                        if QX_SLOTS[g] == s:
-                            x_q[g] = quantize(x_grouped[g], "x%d" % g, keep)
+            vector_part(s, order[order.index("|") + 1 :])

from contextlib import ExitStack

import concourse.mybir as mybir
from concourse.masks import make_identity

F32 = mybir.dt.float32
BF16 = mybir.dt.bfloat16
U32 = mybir.dt.uint32
U8 = mybir.dt.uint8
FP8X4 = mybir.dt.float8_e4m3fn_x4
ACT = mybir.ActivationFunctionType
ALU = mybir.AluOpType

TOKENS, D, DFF, R = 512, 1024, 4096, 512
P = 128
CHUNK = 512
HALF = 256
N_CHUNKS = DFF // CHUNK
FLOPS = 2 * D * DFF * R + 2 * TOKENS * DFF * D
N_SLOTS = 4 * N_CHUNKS

LAGS = (9,) * 8
LAG = 9
A_TV = 4
D_CW = 1
D_CV = 0
D_QV = 2
QW_SLOTS = ((3, 7), (3, 7), (3, 7), (3, 7), (3, 7), (3, 7), (3, 7), (3, 7))
D_ADD = 1
D_G = 2
X_SLOTS = (2, 3)
D_CX = 1
QX_SLOTS = (5, 6)
VEC_W = ((3,), (3,), (3,), (3,), (3,), (3,), (3,), (3,))
VEC_V = ((), (0, 1), (1,), (0, 1), (1,), (0, 1), (1,), (0, 1))
VEC_X = (0,)
DVE_ORDERS = (("cw", "add", "cv", "cx", "ord", "|", "qw", "qv", "qx"),) * 4
W1_BUFS = 0
ORD_V = {}
FUSE_U = False
QW_REV = False
U0_ONE = False
V0_ONE = False
VI_BANKS = ((),) * 8
STORE_SINGLES = 12
WARM = {}
ORD_X = {}
ACT_ORDER = ("cw", "cv", "cx", "ord", "gelu")
HEAD_U0 = (False, False)
HEAD_V0 = (False, False)
HEAD_U1 = (False, False)
QV0_HALVES = True
BIAS_FIRST = 2
GP_BANKS = ((3,), (3,), (3,), (3,), (3,), (3,), (2, 3), (3,))
WQ_BUFS = 8
SPLIT_LAST = 1
U0_QUARTERS = True
EP_BUFS = 7
BIAS_AHEAD = 14
TV1_SLOT = 0
TV2_SLOT = 4
T_AFTER = False
SINGLES = 12


def tile_hybridsuperlayer_pa_kernel(tc, x, c_fc_U, c_fc_S, c_fc_V, c_fc_bias, out):
    nc = tc.nc
    x_rows = x.flatten_outer_dims()
    out_rows = out.flatten_outer_dims()
    u_view = c_fc_U.rearrange("(g m t) r -> g m t r", g=2, t=4)
    v_halves = c_fc_V.rearrange("(c h p j) r -> c h p j r", c=N_CHUNKS, h=2, j=2)
    v_view = c_fc_V.rearrange("(c p j) r -> c p j r", c=N_CHUNKS, j=4)
    x_view = x_rows.rearrange("(p j) d -> p j d", j=4)
    out_view = out_rows.rearrange("(p j) f -> j p f", j=4)

    with ExitStack() as ctx:
        keep = ctx.enter_context(tc.tile_pool(name="keep", bufs=1))
        vg_pool = ctx.enter_context(tc.tile_pool(name="vg", bufs=2))
        vq_pool = ctx.enter_context(tc.tile_pool(name="vq", bufs=3))
        wq_pool = ctx.enter_context(tc.tile_pool(name="wq", bufs=WQ_BUFS))
        w1_pool = ctx.enter_context(tc.tile_pool(name="w1", bufs=W1_BUFS)) if W1_BUFS else wq_pool
        ord_pool = ctx.enter_context(tc.tile_pool(name="ord", bufs=2)) if (ORD_V or ORD_X) else keep
        wf_pool = ctx.enter_context(tc.tile_pool(name="wf", bufs=3))
        ep_pool = ctx.enter_context(tc.tile_pool(name="ep", bufs=EP_BUFS))
        psum = ctx.enter_context(tc.psum_pool(name="psum", bufs=8))
        ctx.enter_context(tc.manual_schedule())

        ident = keep.tile([P, P], F32)
        make_identity(nc, ident[:])
        warm_in = keep.tile([P, 1], F32)
        warm_out = keep.tile([P, 1], F32)
        nc.vector.memset(warm_in[:], 0.0)
        zeros = keep.tile([P, CHUNK], BF16, name="zeros") if WARM else None
        if WARM:
            nc.vector.memset(zeros[:], 0.0)
        nc.scalar.activation(out=warm_out[:], in_=warm_in[:], func=ACT.Gelu)

        s4 = keep.tile([P, 1, 4], BF16)
        u_raw = [keep.tile([P, 4, R], BF16, name="u_raw%d" % g) for g in range(2)]
        v_raw = [keep.tile([P, 4, R], BF16, name="v_raw%d" % c) for c in range(N_CHUNKS)]
        x_raw = keep.tile([P, 4, D], BF16)
        bias_bc = [keep.tile([P, CHUNK], BF16, name="bias_bc%d" % c) for c in range(N_CHUNKS)]

        def load_v(c):
            if c == 0 and not V0_ONE:
                for h in range(2):
                    nc.sync.dma_start(out=v_raw[c][:, 2 * h : 2 * h + 2, :], in_=v_halves[c][h])
            else:
                nc.sync.dma_start(out=v_raw[c][:], in_=v_view[c])

        def load_bias(c):
            nc.sync.dma_start(out=bias_bc[c][:], in_=c_fc_bias[c * CHUNK : (c + 1) * CHUNK].partition_broadcast(P))

        if U0_ONE:
            nc.sync.dma_start(out=u_raw[0][:], in_=u_view[0])
        elif U0_QUARTERS:
            for t in range(2):
                nc.sync.dma_start(out=u_raw[0][:, t : t + 1, :], in_=u_view[0][:, t : t + 1, :])
            nc.sync.dma_start(out=u_raw[0][:, 2:4, :], in_=u_view[0][:, 2:4, :])
        else:
            for h in range(2):
                nc.sync.dma_start(out=u_raw[0][:, 2 * h : 2 * h + 2, :], in_=u_view[0][:, 2 * h : 2 * h + 2, :])
        nc.sync.dma_start(out=s4[:, 0, :], in_=c_fc_S.rearrange("(p t) -> p t", t=4))
        load_v(0)
        nc.sync.dma_start(out=u_raw[1][:], in_=u_view[1])
        load_v(1)
        for h in range(2):
            nc.sync.dma_start(out=x_raw[:, 2 * h : 2 * h + 2, :], in_=x_view[:, 2 * h : 2 * h + 2, :])
        load_v(2)
        load_v(3)
        load_v(4)
        load_v(5)
        load_v(6)
        load_v(7)
        for c in range(BIAS_FIRST):
            load_bias(c)

        def copy_out(on_vector, dst, src):
            if on_vector:
                nc.vector.tensor_copy(out=dst, in_=src)
            else:
                nc.scalar.copy(out=dst, in_=src)

        def transpose_bank(words, warm_passes=0):
            bank = psum.tile([P, 2, 2, P], F32, tag="bank", name="tp_bank")
            for i in range(warm_passes):
                nc.tensor.matmul(out=bank[:].rearrange("p s u m -> p (s u m)"), lhsT=zeros[:, 0:P], rhs=zeros[:], start=True, stop=True)
            for s in range(2):
                for u in range(2):
                    nc.tensor.transpose(bank[:, s, u, :], words[s][u], ident[:])
            return bank

        def every_2nd_word(row_tile, first_word):
            words = row_tile.bitcast(F32)
            return [words[:, first_word + u : first_word + 256 : 2] for u in range(2)]

        def quantize(grouped, name, pool):
            codes = pool.tile([P, CHUNK], U32, tag=name + "_codes", name=name + "_codes", align_bytes=64)
            scales = pool.tile([P, CHUNK], U8, tag=name + "_scales", name=name + "_scales", align_bytes=64)
            nc.vector.quantize_mx(out=codes[:].bitcast(FP8X4), scales=scales[:], in_=grouped[:])
            return codes, scales

        u_grouped = [keep.tile([P, 4 * CHUNK], BF16, name="u_grouped%d" % g, align_bytes=64) for g in range(2)]
        us_grouped = [keep.tile([P, 4 * CHUNK], BF16, name="us_grouped%d" % g, align_bytes=64) for g in range(2)]
        x_grouped = [keep.tile([P, 4 * CHUNK], BF16, name="x_grouped%d" % g, align_bytes=64) for g in range(2)]
        us_q = {}
        x_q = {}
        v_grouped = {}
        v_q = {}
        w_grouped = {}
        w_q = {}
        h_tiles = {}
        banks = {}
        w_flat = {}
        x_ord = {}
        o_pairs = {}
        v_ord = {}

        def scale_u(g, h):
            cols = slice(1024 * h, 1024 * (h + 1))
            nc.vector.tensor_tensor(
                out=us_grouped[g][:, cols].rearrange("p (m t) -> p m t", t=4),
                in0=u_grouped[g][:, cols].rearrange("p (m t) -> p m t", t=4),
                in1=s4[:].to_broadcast([P, HALF, 4]),
                op=ALU.mult,
            )

        def grouped_half(grouped, h):
            return grouped[:, 1024 * h : 1024 * (h + 1)].bitcast(F32).rearrange("p (s m u) -> p s m u", s=2, u=2)

        def tu(g):
            for h in range(2):
                banks[("u", g, h)] = transpose_bank([every_2nd_word(u_raw[g][:, 2 * h + s, :], 0) for s in range(2)], WARM.get(("u", g, h), 0))

        def cu(g, h, on_vector):
            copy_out(on_vector, grouped_half(u_grouped[g], h), banks[("u", g, h)][:].rearrange("p s u m -> p s m u"))

        def order_words(on_vector, dst, src):
            copy_out(on_vector, dst[:], src.bitcast(F32).rearrange("p j (m u) -> p j u m", u=2))

        def ox(g, on_vector):
            x_ord[g] = ord_pool.tile([P, 4, 2, P], F32, tag="x_ord", name="x_ord")
            order_words(on_vector, x_ord[g], x_raw[:, :, 512 * g : 512 * (g + 1)])

        def ov(c, on_vector):
            v_ord[c] = ord_pool.tile([P, 4, 2, P], F32, tag="v_ord", name="v_ord")
            order_words(on_vector, v_ord[c], v_raw[c][:])

        def cus(g, h):
            for s in range(2):
                first = 1024 * h + 512 * s
                nc.vector.tensor_tensor(
                    out=us_grouped[g][:, first : first + 512].rearrange("p (m u e) -> p m u e", u=2, e=2),
                    in0=banks[("u", g, h)][:, s, :, :].bitcast(BF16).rearrange("p u (m e) -> p m u e", e=2),
                    in1=s4[:].rearrange("p o (u e) -> p o u e", u=2).to_broadcast([P, P, 2, 2]),
                    op=ALU.mult,
                )

        def tx(g):
            for h in range(2):
                if g in ORD_X:
                    banks[("x", g, h)] = transpose_bank([[x_ord[g][:, 2 * h + s, u, :] for u in range(2)] for s in range(2)])
                else:
                    banks[("x", g, h)] = transpose_bank([every_2nd_word(x_raw[:, 2 * h + s, :], 256 * g) for s in range(2)])

        def cx(g, h, on_vector):
            copy_out(on_vector, grouped_half(x_grouped[g], h), banks[("x", g, h)][:].rearrange("p s u m -> p s m u"))

        def tv(c):
            v_grouped[c] = vg_pool.tile([P, 4 * CHUNK], BF16, tag="v_grouped", name="v_grouped", align_bytes=64)
            for h in range(2):
                if c in ORD_V:
                    banks[("v", c, h)] = transpose_bank([[v_ord[c][:, 2 * h + j, u, :] for u in range(2)] for j in range(2)])
                else:
                    banks[("v", c, h)] = transpose_bank([every_2nd_word(v_raw[c][:, 2 * h + j, :], 0) for j in range(2)], WARM.get(("v", c, h), 0))

        def cv(c, h, on_vector):
            if c == 0 and not V0_ONE:
                dst = v_grouped[c][:, 1024 * h : 1024 * (h + 1)].bitcast(F32).rearrange("k (p j u) -> k p j u", j=2, u=2)
            else:
                dst = v_grouped[c][:].bitcast(F32).rearrange("k (p j u) -> k p j u", j=4, u=2)[:, :, 2 * h : 2 * h + 2, :]
            copy_out(on_vector, dst, banks[("v", c, h)][:].rearrange("k j u p -> k p j u"))

        def s1(n):
            c, g, h = n // 4, (n % 4) // 2, n % 2
            u_codes, u_scales = us_q[g]
            v_codes, v_scales = v_q[c]
            w_bank = psum.tile([P, 4, HALF], BF16, tag="bank", name="w_bank")
            cols = slice(h * HALF, (h + 1) * HALF)
            for t in range(4):
                d_cols = slice(t * P, (t + 1) * P)
                nc.tensor.matmul_mx(
                    out=w_bank[:, t, :],
                    lhsT=u_codes[:, d_cols].bitcast(FP8X4),
                    lhsT_scale=u_scales[:, d_cols],
                    rhs=v_codes[:, cols].bitcast(FP8X4),
                    rhs_scale=v_scales[:, cols],
                    start=True,
                    stop=True,
                )
            banks[("w", n)] = w_bank

        def cw(n, on_vector):
            c, g, h = n // 4, (n % 4) // 2, n % 2
            if h == 0:
                w_grouped[(c, g)] = (wq_pool, w1_pool)[g].tile([P, 4 * CHUNK], BF16, tag="w_grouped", name="w_grouped", align_bytes=64)
            dst = w_grouped[(c, g)][:, 4 * HALF * h : 4 * HALF * (h + 1)].rearrange("p (f t) -> p f t", t=4)
            if n % 4 in GP_BANKS[c]:
                w_flat[n] = wf_pool.tile([P, 4, HALF], BF16, tag="w_flat", name="w_flat")
                copy_out(on_vector, w_flat[n][:], banks[("w", n)][:])
            else:
                copy_out(on_vector, dst, banks[("w", n)][:].rearrange("p t f -> p f t"))

        def gi(n):
            c, g, h = n // 4, (n % 4) // 2, n % 2
            dst = w_grouped[(c, g)][:, 4 * HALF * h : 4 * HALF * (h + 1)].rearrange("p (f t) -> p f t", t=4)
            if n % 4 in VI_BANKS[c]:
                nc.vector.tensor_copy(out=dst, in_=w_flat[n][:].rearrange("p t f -> p f t"))
            else:
                nc.gpsimd.tensor_scalar(
                    out=dst, in0=w_flat[n][:].rearrange("p t f -> p f t"), scalar1=1.0, scalar2=0.0, op0=ALU.mult, op1=ALU.add
                )

        def pieces(k):
            return 2 if k >= N_SLOTS - SPLIT_LAST else 1

        def s2(k):
            c, i = k // 4, k % 4
            toks = slice(i * P, (i + 1) * P)
            n = pieces(k)
            width = CHUNK // n
            for j in range(n):
                acc = psum.tile([P, width], F32, tag="bank", name="acc")
                cols = slice(j * width, (j + 1) * width)
                for g in range(2):
                    nc.tensor.matmul_mx(
                        out=acc[:],
                        lhsT=x_q[g][0][:, toks].bitcast(FP8X4),
                        lhsT_scale=x_q[g][1][:, toks],
                        rhs=w_q[(c, g)][0][:, cols].bitcast(FP8X4),
                        rhs_scale=w_q[(c, g)][1][:, cols],
                        start=(g == 0),
                        stop=(g == 1),
                    )
                banks[("a", k, j)] = acc

        out_pairs = out_rows.rearrange("(p j) f -> p j f", j=4)

        def paired(k):
            return k < N_SLOTS - SINGLES

        def add(k):
            c = k // 4
            if paired(k):
                if k % 2 == 0:
                    h_tiles[k // 2] = ep_pool.tile([P, 2, CHUNK], F32, tag="h_sb", name="h_sb")
                nc.vector.tensor_tensor(out=h_tiles[k // 2][:, k % 2, :], in0=banks[("a", k, 0)][:], in1=bias_bc[c][:], op=ALU.add)
                return
            n = pieces(k)
            width = CHUNK // n
            for j in range(n):
                h_tiles[(k, j)] = ep_pool.tile([P, width], F32, tag="h_sb", name="h_sb")
                nc.vector.tensor_tensor(
                    out=h_tiles[(k, j)][:], in0=banks[("a", k, j)][:], in1=bias_bc[c][:, j * width : (j + 1) * width], op=ALU.add
                )

        def gelu(k):
            c, i = k // 4, k % 4
            if paired(k):
                if k % 2 == 1:
                    o_pair = ep_pool.tile([P, 2, CHUNK], F32, tag="o_sb", name="o_sb")
                    nc.scalar.activation(out=o_pair[:], in_=h_tiles[k // 2][:], func=ACT.Gelu)
                    nc.sync.dma_start(out=out_pairs[:, i - 1 : i + 1, c * CHUNK : (c + 1) * CHUNK], in_=o_pair[:])
                return
            if k < N_SLOTS - STORE_SINGLES:
                if k % 2 == 0:
                    o_pairs[k // 2] = ep_pool.tile([P, 2, CHUNK], F32, tag="o_sb", name="o_sb")
                nc.scalar.activation(out=o_pairs[k // 2][:, k % 2, :], in_=h_tiles[(k, 0)][:], func=ACT.Gelu)
                if k % 2 == 1:
                    nc.sync.dma_start(out=out_pairs[:, i - 1 : i + 1, c * CHUNK : (c + 1) * CHUNK], in_=o_pairs[k // 2][:])
                return
            n = pieces(k)
            width = CHUNK // n
            for j in range(n):
                o_sb = ep_pool.tile([P, width], F32, tag="o_sb", name="o_sb")
                nc.scalar.activation(out=o_sb[:], in_=h_tiles[(k, j)][:], func=ACT.Gelu)
                first = c * CHUNK + j * width
                nc.sync.dma_start(out=out_view[i][:, first : first + width], in_=o_sb[:])

        def quantize_v0(h):
            if h == 0:
                v_q[0] = (
                    vq_pool.tile([P, CHUNK], U32, tag="v_codes", name="v_codes", align_bytes=64),
                    vq_pool.tile([P, CHUNK], U8, tag="v_scales", name="v_scales", align_bytes=64),
                )
            cols = slice(HALF * h, HALF * (h + 1))
            nc.vector.quantize_mx(
                out=v_q[0][0][:, cols].bitcast(FP8X4), scales=v_q[0][1][:, cols], in_=v_grouped[0][:, 4 * HALF * h : 4 * HALF * (h + 1)]
            )

        tu(0)
        if FUSE_U:
            cus(0, 0)
            cus(0, 1)
        else:
            cu(0, 0, HEAD_U0[0])
            cu(0, 1, HEAD_U0[1])
            scale_u(0, 0)
            scale_u(0, 1)
        tv(0)
        cv(0, 0, HEAD_V0[0])
        cv(0, 1, HEAD_V0[1])
        us_q[0] = quantize(us_grouped[0], "us0", keep)
        if QV0_HALVES:
            quantize_v0(0)
            quantize_v0(1)
        else:
            v_q[0] = quantize(v_grouped[0], "v", vq_pool)
        tu(1)
        if FUSE_U:
            cus(1, 0)
            cus(1, 1)
        else:
            cu(1, 0, HEAD_U1[0])
            cu(1, 1, HEAD_U1[1])
            scale_u(1, 0)
            scale_u(1, 1)
        us_q[1] = quantize(us_grouped[1], "us1", keep)

        def tv_slot(c):
            return TV1_SLOT if c == 1 else (TV2_SLOT if c == 2 else 4 * c - A_TV)

        def tiles_at(slot):
            return [k for k in range(N_SLOTS) if k + LAGS[k // 4] == slot]

        def vector_part(s, kinds):
            for what in kinds:
                if what == "ord":
                    for g in sorted(ORD_X):
                        if ORD_X[g] == (s, True):
                            ox(g, True)
                    for c in sorted(ORD_V):
                        if ORD_V[c] == (s, True):
                            ov(c, True)
                if what == "add":
                    for k in tiles_at(s - D_ADD):
                        add(k)
                if what == "cw" and 0 <= s - D_CW < N_SLOTS and (s - D_CW) % 4 in VEC_W[(s - D_CW) // 4]:
                    cw(s - D_CW, True)
                if what == "cv":
                    for c in range(1, N_CHUNKS):
                        if tv_slot(c) + D_CV == s:
                            for h in VEC_V[c]:
                                cv(c, h, True)
                if what == "cx":
                    for g in range(2):
                        if X_SLOTS[g] + D_CX == s:
                            for h in VEC_X:
                                cx(g, h, True)
                if what == "qw":
                    for c in (list(reversed(range(N_CHUNKS))) if QW_REV else list(range(N_CHUNKS))):
                        for g in range(2):
                            if 4 * c + QW_SLOTS[c][g] == s:
                                w_q[(c, g)] = quantize(w_grouped[(c, g)], "w", wq_pool)
                if what == "qv":
                    for c in range(1, N_CHUNKS):
                        if tv_slot(c) + D_QV == s:
                            v_q[c] = quantize(v_grouped[c], "v", vq_pool)
                if what == "qx":
                    for g in range(2):
                        if QX_SLOTS[g] == s:
                            x_q[g] = quantize(x_grouped[g], "x%d" % g, keep)

        for s in range(N_SLOTS + LAG + D_G + 2):
            for c in range(BIAS_FIRST, N_CHUNKS):
                if 4 * c + LAG - BIAS_AHEAD == s:
                    load_bias(c)
            def t_runs():
                for c in range(1, N_CHUNKS):
                    if tv_slot(c) == s:
                        tv(c)
                for g in range(2):
                    if X_SLOTS[g] == s:
                        tx(g)
            if not T_AFTER:
                t_runs()
            if s < N_SLOTS:
                s1(s)
            for k in tiles_at(s):
                s2(k)
            if T_AFTER:
                t_runs()
            order = DVE_ORDERS[s % 4]
            vector_part(s, order[: order.index("|")])
            for what in ACT_ORDER:
                if what == "ord":
                    for g in sorted(ORD_X):
                        if ORD_X[g] == (s, False):
                            ox(g, False)
                    for c in sorted(ORD_V):
                        if ORD_V[c] == (s, False):
                            ov(c, False)
                if what == "gelu":
                    for k in tiles_at(s - D_G):
                        gelu(k)
                if what == "cw" and 0 <= s - D_CW < N_SLOTS and (s - D_CW) % 4 not in VEC_W[(s - D_CW) // 4]:
                    cw(s - D_CW, False)
                if what == "cv":
                    for c in range(1, N_CHUNKS):
                        if tv_slot(c) + D_CV == s:
                            for h in range(2):
                                if h not in VEC_V[c]:
                                    cv(c, h, False)
                if what == "cx":
                    for g in range(2):
                        if X_SLOTS[g] + D_CX == s:
                            for h in range(2):
                                if h not in VEC_X:
                                    cx(g, h, False)
            if 0 <= s - D_CW < N_SLOTS and (s - D_CW) % 4 in GP_BANKS[(s - D_CW) // 4]:
                gi(s - D_CW)
            vector_part(s, order[order.index("|") + 1 :])
